import numpy as np
import ml_dtypes


def mxq(x, axis, fmt="e4m3"):
    dtype, down = {"e4m3": (ml_dtypes.float8_e4m3fn, 7), "e5m2": (ml_dtypes.float8_e5m2, 14)}[fmt]
    v = np.moveaxis(np.asarray(x, np.float32).astype(ml_dtypes.bfloat16).astype(np.float64), axis, -1)
    blocks = v.reshape(v.shape[:-1] + (-1, 32))
    amax = np.abs(blocks).max(-1, keepdims=True)
    byte = np.maximum(np.where(amax > 0, np.frexp(amax)[1] - 1 + 127, 0) - down, 1)
    scale = np.exp2(byte - 127.0)
    codes = (blocks / scale).astype(np.float32).astype(dtype).astype(np.float64)
    return np.moveaxis((codes * scale).reshape(v.shape), -1, axis)


WIDE = False


def mx_kscale(k):
    if not WIDE:
        return np.ones(k)
    levels = np.array([10, -10, 5, -5, 0])
    a = np.random.permutation(np.resize(levels, k // 512 * 4)).reshape(k // 512, 4)
    idx = np.arange(k)
    return np.exp2(a[idx // 512, idx % 128 // 32])


BF16 = ml_dtypes.bfloat16


def bf(x):
    return np.asarray(x, np.float32).astype(BF16)


def f64(x):
    return np.asarray(x).astype(np.float64)


B, C, W, H = 8, 512, 16, 32


def spatial_shift1(y):
    cq = y.shape[-1] // 4
    p0 = np.concatenate([y[:, :1, :, 0 * cq:1 * cq], y[:, :-1, :, 0 * cq:1 * cq]], axis=1)
    p1 = np.concatenate([y[:, 1:, :, 1 * cq:2 * cq], y[:, -1:, :, 1 * cq:2 * cq]], axis=1)
    p2 = np.concatenate([y[:, :, :1, 2 * cq:3 * cq], y[:, :, :-1, 2 * cq:3 * cq]], axis=2)
    p3 = np.concatenate([y[:, :, 1:, 3 * cq:], y[:, :, -1:, 3 * cq:]], axis=2)
    return np.concatenate([p0, p1, p2, p3], axis=-1)


def spatial_shift2(y):
    cq = y.shape[-1] // 4
    p0 = np.concatenate([y[:, :, :1, 0 * cq:1 * cq], y[:, :, :-1, 0 * cq:1 * cq]], axis=2)
    p1 = np.concatenate([y[:, :, 1:, 1 * cq:2 * cq], y[:, :, -1:, 1 * cq:2 * cq]], axis=2)
    p2 = np.concatenate([y[:, :1, :, 2 * cq:3 * cq], y[:, :-1, :, 2 * cq:3 * cq]], axis=1)
    p3 = np.concatenate([y[:, 1:, :, 3 * cq:], y[:, -1:, :, 3 * cq:]], axis=1)
    return np.concatenate([p0, p1, p2, p3], axis=-1)


def setup_inputs():
    s = mx_kscale(C)
    return {"x": bf(np.random.standard_normal((B, C, W, H)) * s[None, :, None, None]),
            "w1": bf(np.random.standard_normal((3 * C, C)) / np.sqrt(C) / s[None, :]),
            "b1": bf(np.random.standard_normal(3 * C) * 0.1)}


def reference(x, w1, b1):
    xp = f64(x).transpose(0, 2, 3, 1)
    y = (mxq(xp, 3, "e4m3") @ mxq(f64(w1), 1, "e4m3").T) + f64(b1)
    x1 = spatial_shift1(y[..., :C])
    x2 = spatial_shift2(y[..., C:2 * C])
    x3 = y[..., 2 * C:]
    a = np.sum(x1 + x2 + x3, axis=(1, 2))
    return x1, x2, x3, a

@@ -1,0 +1,233 @@
+import concourse.mybir as mybir
+from concourse.masks import make_identity
+
+FP8X4 = mybir.dt.float8_e4m3fn_x4
+BF16 = mybir.dt.bfloat16
+F32 = mybir.dt.float32
+U32 = mybir.dt.uint32
+U8 = mybir.dt.uint8
+ADD = mybir.AluOpType.add
+MULT = mybir.AluOpType.mult
+AX = mybir.AxisListType.X
+
+P = 128
+FLOPS = 2 * 4096 * 512 * 1536
+
+NHO = 4
+SLOT = 64
+PLANE = 18 * SLOT
+CV = 88
+
+ROFPOS = [0, 6, 4, 2, 1, 7, 5, 3, 8, 10, 9, 11]
+WM, HM, WP, HP, ZZ = 0, 256, 512, 768, 1024
+
+
+def tile_modelnew_pa_t_kernel(tc, x, w1, b1, out_0, out_1, out_2, out_3):
+    nc = tc.nc
+    outs = [out_0, out_1, out_2]
+    with tc.tile_pool(name="const", bufs=1) as const, tc.tile_pool(name="wpool", bufs=1) as wpool, tc.tile_pool(
+        name="xpool", bufs=1
+    ) as xpool, tc.tile_pool(name="stage", bufs=2) as stage, tc.psum_pool(name="acc", bufs=1) as accp, tc.psum_pool(
+        name="mm", bufs=6
+    ) as mmp:
+        brow = const.tile([P, 1536], BF16)
+        nc.gpsimd.memset(brow[:], 0.0)
+        nc.sync.dma_start(out=brow[0:1, :], in_=b1.unsqueeze(0))
+        w_sb = wpool.tile([P, 12 * 512], BF16)
+        for i in range(3):
+            nc.sync.dma_start(
+                out=w_sb[:, i * 2048 : (i + 1) * 2048].rearrange("p (r k) -> p r k", k=512),
+                in_=w1[i * 512 : (i + 1) * 512, :].rearrange("(r p) k -> p r k", p=P),
+            )
+        raw = xpool.tile([P, 8, 2048], BF16)
+        for b in range(8):
+            nc.sync.dma_start(out=raw[:, b, :], in_=x[b].rearrange("(p j) w h -> p (j w h)", j=4))
+
+        ident = const.tile([P, P], F32)
+        make_identity(nc, ident[:])
+        ones_bf = const.tile([P, P], BF16)
+        nc.vector.memset(ones_bf[:], 1.0)
+        ind = const.tile([P, P], F32)
+        nc.vector.memset(ind[:], 0.0)
+        nc.vector.tensor_reduce(out=ind[:, 0:8], in_=ident[:].rearrange("p (r m) -> p m r", m=8), axis=AX, op=ADD)
+
+        bias = const.tile([P, 1536], F32)
+        for i in range(3):
+            pb = mmp.tile([P, 512], F32, tag="mm")
+            nc.tensor.matmul(pb[:], lhsT=ones_bf[:], rhs=brow[:, i * 512 : (i + 1) * 512], start=True, stop=True)
+            nc.vector.tensor_copy(out=bias[:, i * 512 : (i + 1) * 512], in_=pb[:])
+        bsum = const.tile([P, 512], F32)
+        nc.vector.tensor_tensor(out=bsum[:], in0=bias[:, 0:512], in1=bias[:, 512:1024], op=ADD)
+        nc.vector.tensor_tensor(out=bsum[:], in0=bsum[:], in1=bias[:, 1024:1536], op=ADD)
+
+        w32 = w_sb[:].bitcast(F32).rearrange("p (r q u) -> p r u q", r=12, u=2)
+        gw = wpool.tile([P, 6144], BF16, align_bytes=64)
+        gw32 = gw[:].bitcast(F32).rearrange("p (i r o u) -> p i r o u", i=6, r=2, u=2)
+        wcodes = wpool.tile([P, 1536], U32, align_bytes=64)
+        wscales = wpool.tile([P, 1536], U8, align_bytes=64)
+        for i in range(6):
+            pt = mmp.tile([P, 2, 2, P], F32, tag="mm")
+            for rr in range(2):
+                for u in range(2):
+                    nc.tensor.transpose(pt[:, rr, u, :], w32[:, ROFPOS[2 * i + rr], u, :], ident[:])
+            src = pt[:].rearrange("p r u o -> p r o u")
+            if i % 2 == 0:
+                nc.vector.tensor_copy(out=gw32[:, i], in_=src)
+            else:
+                nc.scalar.copy(out=gw32[:, i], in_=src)
+        for i in range(3):
+            nc.vector.quantize_mx(
+                out=wcodes[:, i * 512 : (i + 1) * 512].bitcast(FP8X4),
+                scales=wscales[:, i * 512 : (i + 1) * 512],
+                in_=gw[:, i * 2048 : (i + 1) * 2048],
+            )
+
+        gx = xpool.tile([P, NHO, PLANE, 4], BF16, align_bytes=64)
+        gxb = gx[:, :, SLOT : SLOT + 1024, :].rearrange("p o (c b) j -> p b c j o", b=8)
+        for b in range(8):
+            src = raw[:, b, :].rearrange("p (j c o) -> p c j o", j=4, o=NHO)
+            nc.vector.tensor_copy(out=gxb[:, b, 0:CV], in_=src[:, 0:CV])
+            nc.scalar.copy(out=gxb[:, b, CV:P], in_=src[:, CV:P])
+        nc.vector.tensor_copy(out=gx[:, :, 0:SLOT, :], in_=gx[:, :, SLOT : 2 * SLOT, :])
+        nc.scalar.copy(out=gx[:, :, 17 * SLOT : 18 * SLOT, :], in_=gx[:, :, 16 * SLOT : 17 * SLOT, :])
+        hx = xpool.tile([P, 4, 2, 256, 4], BF16, align_bytes=64)
+        g0 = gx[:, 0, SLOT : SLOT + 1024, :].rearrange("p (q v r) j -> p q v (r j)", q=4, v=4)
+        g3 = gx[:, 3, SLOT : SLOT + 1024, :].rearrange("p (q v r) j -> p q v (r j)", q=4, v=4)
+        hm = hx[:, :, 0].rearrange("p q (v r) j -> p q v (r j)", v=4)
+        hp = hx[:, :, 1].rearrange("p q (v r) j -> p q v (r j)", v=4)
+        nc.vector.tensor_copy(out=hm[:, :, :, 32:256], in_=g3[:, :, :, 0:224])
+        nc.vector.tensor_copy(out=hm[:, :, :, 0:32], in_=g0[:, :, :, 0:32])
+        nc.vector.tensor_copy(out=hp[:, :, :, 0:224], in_=g0[:, :, :, 32:256])
+        nc.vector.tensor_copy(out=hp[:, :, :, 224:256], in_=g3[:, :, :, 224:256])
+
+        xcodes = xpool.tile([P, NHO, PLANE], U32, align_bytes=64)
+        xscales = xpool.tile([P, NHO, PLANE], U8, align_bytes=64)
+        hcodes = xpool.tile([P, 4, 512], U32, align_bytes=64)
+        hscales = xpool.tile([P, 4, 512], U8, align_bytes=64)
+
+        def quantise_chunk(q):
+            lo = q * 256
+            hi = min(lo + 256, PLANE)
+            for ho in range(NHO):
+                nc.vector.quantize_mx(
+                    out=xcodes[:, ho, lo:hi].bitcast(FP8X4),
+                    scales=xscales[:, ho, lo:hi],
+                    in_=gx[:, ho, lo:hi, :].rearrange("p c j -> p (c j)"),
+                )
+
+        def quantise_halo(q):
+            nc.vector.quantize_mx(
+                out=hcodes[:, q, :].bitcast(FP8X4),
+                scales=hscales[:, q, :],
+                in_=hx[:, q].rearrange("p s c j -> p (s c j)"),
+            )
+
+        def lhs(kind, wp, ho):
+            o0 = (2 * wp + 1) * SLOT
+            if kind == "wm":
+                return xcodes[:, ho, o0 - SLOT : o0 + SLOT], xscales[:, ho, o0 - SLOT : o0 + SLOT]
+            if kind == "wp":
+                return xcodes[:, ho, o0 + SLOT : o0 + 3 * SLOT], xscales[:, ho, o0 + SLOT : o0 + 3 * SLOT]
+            if kind == "hm" and ho == 0:
+                c0 = (wp % 2) * P
+                return hcodes[:, wp // 2, c0 : c0 + P], hscales[:, wp // 2, c0 : c0 + P]
+            if kind == "hp" and ho == NHO - 1:
+                c0 = 256 + (wp % 2) * P
+                return hcodes[:, wp // 2, c0 : c0 + P], hscales[:, wp // 2, c0 : c0 + P]
+            pl = ho
+            if kind == "hm":
+                pl = ho - 1
+            if kind == "hp":
+                pl = ho + 1
+            return xcodes[:, pl, o0 : o0 + P], xscales[:, pl, o0 : o0 + P]
+
+        def mx(out, lc, ls, col, n, start, stop):
+            nc.tensor.matmul_mx(
+                out=out,
+                lhsT=lc.bitcast(FP8X4),
+                lhsT_scale=ls,
+                rhs=wcodes[:, col : col + n].bitcast(FP8X4),
+                rhs_scale=wscales[:, col : col + n],
+                start=start,
+                stop=stop,
+            )
+
+        s1 = accp.tile([P, 256], F32)
+        s2 = accp.tile([P, 256], F32)
+
+        quantise_chunk(0)
+        quantise_halo(0)
+        for wp in range(8):
+            if wp == 0:
+                quantise_chunk(1)
+            elif wp % 2 == 1:
+                if wp < 7:
+                    quantise_halo((wp + 1) // 2)
+                    quantise_chunk((wp + 3) // 2)
+            st1 = stage.tile([P, NHO, 512], F32)
+            st2 = stage.tile([P, NHO, 512], F32)
+            st3 = stage.tile([P, NHO, 512], F32)
+            for ho in range(NHO):
+                first = wp == 0 and ho == 0
+                last = wp == 7 and ho == NHO - 1
+                p1 = mmp.tile([P, 512], F32, tag="mm")
+                p2 = mmp.tile([P, 512], F32, tag="mm")
+                p3 = mmp.tile([P, 512], F32, tag="mm")
+                lc, ls = lhs("z", wp, ho)
+                mx(p3[:], lc, ls, ZZ, 512, True, True)
+                mx(s1[:], lc, ls, ZZ, 256, first, False)
+                mx(s2[:], lc, ls, ZZ + 256, 256, first, False)
+                lc, ls = lhs("wm", wp, ho)
+                mx(p1[:, 0:128], lc, ls, WM, 128, True, True)
+                mx(p2[:, 256:384], lc, ls, WM + 128, 128, True, True)
+                mx(s1[:], lc, ls, WM, 256, False, False)
+                lc, ls = lhs("wp", wp, ho)
+                mx(p1[:, 128:256], lc, ls, WP, 128, True, True)
+                mx(p2[:, 384:512], lc, ls, WP + 128, 128, True, True)
+                mx(s2[:], lc, ls, WP, 256, False, False)
+                lc, ls = lhs("hm", wp, ho)
+                mx(p2[:, 0:128], lc, ls, HM, 128, True, True)
+                mx(p1[:, 256:384], lc, ls, HM + 128, 128, True, True)
+                mx(s1[:], lc, ls, HM, 256, False, last)
+                lc, ls = lhs("hp", wp, ho)
+                mx(p2[:, 128:256], lc, ls, HP, 128, True, True)
+                mx(p1[:, 384:512], lc, ls, HP + 128, 128, True, True)
+                mx(s2[:], lc, ls, HP, 256, False, last)
+                nc.scalar.copy(
+                    out=st3[:, ho, :].rearrange("p (a b c) -> p a b c", a=2, b=2),
+                    in_=p3[:].rearrange("p (a b c) -> p b a c", a=2, b=2),
+                )
+                nc.vector.tensor_tensor(out=st1[:, ho, :], in0=p1[:], in1=bias[:, 0:512], op=ADD)
+                if ho == NHO - 1:
+                    nc.scalar.copy(out=st2[:, ho, :], in_=p2[:])
+                    nc.gpsimd.tensor_tensor(out=st2[:, ho, :], in0=st2[:, ho, :], in1=bias[:, 512:1024], op=ADD)
+                else:
+                    nc.vector.tensor_tensor(out=st2[:, ho, :], in0=p2[:], in1=bias[:, 512:1024], op=ADD)
+            nc.gpsimd.tensor_tensor(
+                out=st3[:],
+                in0=st3[:],
+                in1=bias[:, 1024:1536].unsqueeze(1).to_broadcast([P, NHO, 512]),
+                op=ADD,
+            )
+            for k, st in enumerate([st1, st2, st3]):
+                nc.sync.dma_start(
+                    out=outs[k][:, 2 * wp : 2 * wp + 2, :, :].rearrange("b w (i o) c -> (w i) b (o c)", o=NHO),
+                    in_=st[:].rearrange("p o c -> p (o c)"),
+                )
+
+        ssb = const.tile([P, 512], F32)
+        ssv = ssb[:].rearrange("p (a b c) -> p b a c", a=2, b=2)
+        nc.vector.tensor_copy(out=ssv[:, 0], in_=s1[:].rearrange("p (a c) -> p a c", a=2))
+        nc.scalar.copy(out=ssv[:, 1], in_=s2[:].rearrange("p (a c) -> p a c", a=2))
+        pa = mmp.tile([P, 512], F32, tag="mm")
+        nc.tensor.matmul(pa[:], lhsT=ind[:], rhs=ssb[:], start=True, stop=True)
+        a_sb = const.tile([P, 512], F32)
+        nc.vector.scalar_tensor_tensor(
+            out=a_sb[:],
+            in0=bsum[:],
+            scalar=512.0,
+            in1=pa[:],
+            op0=MULT,
+            op1=ADD,
+        )
+        nc.sync.dma_start(out=out_3, in_=a_sb[0:8, :])

@@ -16,6 +16,7 @@ FLOPS = 2 * 4096 * 512 * 1536
 NHO = 4
 SLOT = 64
 PLANE = 18 * SLOT
+GS = 2
 CV = 88
 
 ROFPOS = [0, 6, 4, 2, 1, 7, 5, 3, 8, 10, 9, 11]
@@ -193,20 +194,24 @@ def tile_modelnew_pa_t_kernel(tc, x, w1, b1, out_0, out_1, out_2, out_3):
                 mx(p2[:, 128:256], lc, ls, HP, 128, True, True)
                 mx(p1[:, 384:512], lc, ls, HP + 128, 128, True, True)
                 mx(s2[:], lc, ls, HP, 256, False, last)
-                nc.scalar.copy(
-                    out=st3[:, ho, :].rearrange("p (a b c) -> p a b c", a=2, b=2),
-                    in_=p3[:].rearrange("p (a b c) -> p b a c", a=2, b=2),
-                )
-                nc.vector.tensor_tensor(out=st1[:, ho, :], in0=p1[:], in1=bias[:, 0:512], op=ADD)
-                if ho == NHO - 1:
-                    nc.scalar.copy(out=st2[:, ho, :], in_=p2[:])
-                    nc.gpsimd.tensor_tensor(out=st2[:, ho, :], in0=st2[:, ho, :], in1=bias[:, 512:1024], op=ADD)
+                if ho < GS:
+                    nc.scalar.copy(
+                        out=st3[:, ho, :].rearrange("p (a b c) -> p a b c", a=2, b=2),
+                        in_=p3[:].rearrange("p (a b c) -> p b a c", a=2, b=2),
+                    )
                 else:
-                    nc.vector.tensor_tensor(out=st2[:, ho, :], in0=p2[:], in1=bias[:, 512:1024], op=ADD)
+                    nc.vector.tensor_tensor(
+                        out=st3[:, ho, :].rearrange("p (a b c) -> p a b c", a=2, b=2),
+                        in0=p3[:].rearrange("p (a b c) -> p b a c", a=2, b=2),
+                        in1=bias[:, 1024:1536].rearrange("p (a b c) -> p a b c", a=2, b=2),
+                        op=ADD,
+                    )
+                nc.vector.tensor_tensor(out=st1[:, ho, :], in0=p1[:], in1=bias[:, 0:512], op=ADD)
+                nc.vector.tensor_tensor(out=st2[:, ho, :], in0=p2[:], in1=bias[:, 512:1024], op=ADD)
             nc.gpsimd.tensor_tensor(
-                out=st3[:],
-                in0=st3[:],
-                in1=bias[:, 1024:1536].unsqueeze(1).to_broadcast([P, NHO, 512]),
+                out=st3[:, 0:GS, :],
+                in0=st3[:, 0:GS, :],
+                in1=bias[:, 1024:1536].unsqueeze(1).to_broadcast([P, GS, 512]),
                 op=ADD,
             )
             for k, st in enumerate([st1, st2, st3]):

@@ -84,11 +84,11 @@ def tile_modelnew_pa_t_kernel(tc, x, w1, b1, out_0, out_1, out_2, out_3):
             )
 
         gx = xpool.tile([P, NHO, PLANE, 4], BF16, align_bytes=64)
-        gxb = gx[:, :, SLOT : SLOT + 1024, :].rearrange("p o (c b) j -> p b c j o", b=8)
+        gxb = gx[:, :, SLOT : SLOT + 1024, :].rearrange("p o (c b) j -> p b o c j", b=8)
         for b in range(8):
-            src = raw[:, b, :].rearrange("p (j c o) -> p c j o", j=4, o=NHO)
-            nc.vector.tensor_copy(out=gxb[:, b, 0:CV], in_=src[:, 0:CV])
-            nc.scalar.copy(out=gxb[:, b, CV:P], in_=src[:, CV:P])
+            src = raw[:, b, :].rearrange("p (j c o) -> p o c j", j=4, o=NHO)
+            nc.vector.tensor_copy(out=gxb[:, b, :, 0:CV], in_=src[:, :, 0:CV])
+            nc.scalar.copy(out=gxb[:, b, :, CV:P], in_=src[:, :, CV:P])
         nc.vector.tensor_copy(out=gx[:, :, 0:SLOT, :], in_=gx[:, :, SLOT : 2 * SLOT, :])
         nc.scalar.copy(out=gx[:, :, 17 * SLOT : 18 * SLOT, :], in_=gx[:, :, 16 * SLOT : 17 * SLOT, :])
         hx = xpool.tile([P, 4, 2, 256, 4], BF16, align_bytes=64)

@@ -16,7 +16,7 @@ FLOPS = 2 * 4096 * 512 * 1536
 NHO = 4
 SLOT = 64
 PLANE = 18 * SLOT
-GS = 2
+GS = 0
 CV = 88
 
 ROFPOS = [0, 6, 4, 2, 1, 7, 5, 3, 8, 10, 9, 11]
@@ -208,12 +208,13 @@ def tile_modelnew_pa_t_kernel(tc, x, w1, b1, out_0, out_1, out_2, out_3):
                     )
                 nc.vector.tensor_tensor(out=st1[:, ho, :], in0=p1[:], in1=bias[:, 0:512], op=ADD)
                 nc.vector.tensor_tensor(out=st2[:, ho, :], in0=p2[:], in1=bias[:, 512:1024], op=ADD)
-            nc.gpsimd.tensor_tensor(
-                out=st3[:, 0:GS, :],
-                in0=st3[:, 0:GS, :],
-                in1=bias[:, 1024:1536].unsqueeze(1).to_broadcast([P, GS, 512]),
-                op=ADD,
-            )
+            if GS > 0:
+                nc.gpsimd.tensor_tensor(
+                    out=st3[:, 0:GS, :],
+                    in0=st3[:, 0:GS, :],
+                    in1=bias[:, 1024:1536].unsqueeze(1).to_broadcast([P, GS, 512]),
+                    op=ADD,
+                )
             for k, st in enumerate([st1, st2, st3]):
                 nc.sync.dma_start(
                     out=outs[k][:, 2 * wp : 2 * wp + 2, :, :].rearrange("b w (i o) c -> (w i) b (o c)", o=NHO),

@@ -16,7 +16,7 @@ FLOPS = 2 * 4096 * 512 * 1536
 NHO = 4
 SLOT = 64
 PLANE = 18 * SLOT
-GS = 0
+NSTAGE = 8
 CV = 88
 
 ROFPOS = [0, 6, 4, 2, 1, 7, 5, 3, 8, 10, 9, 11]
@@ -28,7 +28,7 @@ def tile_modelnew_pa_t_kernel(tc, x, w1, b1, out_0, out_1, out_2, out_3):
     outs = [out_0, out_1, out_2]
     with tc.tile_pool(name="const", bufs=1) as const, tc.tile_pool(name="wpool", bufs=1) as wpool, tc.tile_pool(
         name="xpool", bufs=1
-    ) as xpool, tc.tile_pool(name="stage", bufs=2) as stage, tc.psum_pool(name="acc", bufs=1) as accp, tc.psum_pool(
+    ) as xpool, tc.tile_pool(name="stage", bufs=NSTAGE) as stage, tc.psum_pool(name="acc", bufs=1) as accp, tc.psum_pool(
         name="mm", bufs=6
     ) as mmp:
         brow = const.tile([P, 1536], BF16)
@@ -96,10 +96,12 @@ def tile_modelnew_pa_t_kernel(tc, x, w1, b1, out_0, out_1, out_2, out_3):
         g3 = gx[:, 3, SLOT : SLOT + 1024, :].rearrange("p (q v r) j -> p q v (r j)", q=4, v=4)
         hm = hx[:, :, 0].rearrange("p q (v r) j -> p q v (r j)", v=4)
         hp = hx[:, :, 1].rearrange("p q (v r) j -> p q v (r j)", v=4)
-        nc.vector.tensor_copy(out=hm[:, :, :, 32:256], in_=g3[:, :, :, 0:224])
-        nc.vector.tensor_copy(out=hm[:, :, :, 0:32], in_=g0[:, :, :, 0:32])
-        nc.vector.tensor_copy(out=hp[:, :, :, 0:224], in_=g0[:, :, :, 32:256])
-        nc.vector.tensor_copy(out=hp[:, :, :, 224:256], in_=g3[:, :, :, 224:256])
+
+        def halo_copies(q0, q1):
+            nc.vector.tensor_copy(out=hm[:, q0:q1, :, 32:256], in_=g3[:, q0:q1, :, 0:224])
+            nc.vector.tensor_copy(out=hm[:, q0:q1, :, 0:32], in_=g0[:, q0:q1, :, 0:32])
+            nc.vector.tensor_copy(out=hp[:, q0:q1, :, 0:224], in_=g0[:, q0:q1, :, 32:256])
+            nc.vector.tensor_copy(out=hp[:, q0:q1, :, 224:256], in_=g3[:, q0:q1, :, 224:256])
 
         xcodes = xpool.tile([P, NHO, PLANE], U32, align_bytes=64)
         xscales = xpool.tile([P, NHO, PLANE], U8, align_bytes=64)
@@ -156,70 +158,66 @@ def tile_modelnew_pa_t_kernel(tc, x, w1, b1, out_0, out_1, out_2, out_3):
         s1 = accp.tile([P, 256], F32)
         s2 = accp.tile([P, 256], F32)
 
+        def store(kk, wp, st):
+            nc.sync.dma_start(
+                out=outs[kk][:, 2 * wp : 2 * wp + 2, :, :].rearrange("b w (i o) c -> (w i) b (o c)", o=NHO),
+                in_=st[:].rearrange("p o c -> p (o c)"),
+            )
+
         quantise_chunk(0)
+        halo_copies(0, 1)
         quantise_halo(0)
+        quantise_chunk(1)
+        halo_copies(1, 4)
         for wp in range(8):
-            if wp == 0:
-                quantise_chunk(1)
-            elif wp % 2 == 1:
-                if wp < 7:
-                    quantise_halo((wp + 1) // 2)
-                    quantise_chunk((wp + 3) // 2)
-            st1 = stage.tile([P, NHO, 512], F32)
-            st2 = stage.tile([P, NHO, 512], F32)
-            st3 = stage.tile([P, NHO, 512], F32)
+            if wp % 2 == 1 and wp < 7:
+                quantise_halo((wp + 1) // 2)
+                quantise_chunk((wp + 3) // 2)
+            st = stage.tile([P, NHO, 512], F32, tag="st")
             for ho in range(NHO):
-                first = wp == 0 and ho == 0
-                last = wp == 7 and ho == NHO - 1
-                p1 = mmp.tile([P, 512], F32, tag="mm")
-                p2 = mmp.tile([P, 512], F32, tag="mm")
-                p3 = mmp.tile([P, 512], F32, tag="mm")
+                pm = mmp.tile([P, 512], F32, tag="mm")
                 lc, ls = lhs("z", wp, ho)
-                mx(p3[:], lc, ls, ZZ, 512, True, True)
+                first = wp == 0 and ho == 0
+                mx(pm[:], lc, ls, ZZ, 512, True, True)
                 mx(s1[:], lc, ls, ZZ, 256, first, False)
                 mx(s2[:], lc, ls, ZZ + 256, 256, first, False)
+                nc.scalar.copy(
+                    out=st[:, ho, :].rearrange("p (a b c) -> p a b c", a=2, b=2),
+                    in_=pm[:].rearrange("p (a b c) -> p b a c", a=2, b=2),
+                )
+                nc.gpsimd.tensor_tensor(out=st[:, ho, :], in0=st[:, ho, :], in1=bias[:, 1024:1536], op=ADD)
+            store(2, wp, st)
+            st = stage.tile([P, NHO, 512], F32, tag="st")
+            for ho in range(NHO):
+                pm = mmp.tile([P, 512], F32, tag="mm")
                 lc, ls = lhs("wm", wp, ho)
-                mx(p1[:, 0:128], lc, ls, WM, 128, True, True)
-                mx(p2[:, 256:384], lc, ls, WM + 128, 128, True, True)
+                mx(pm[:, 0:128], lc, ls, WM, 128, True, True)
                 mx(s1[:], lc, ls, WM, 256, False, False)
                 lc, ls = lhs("wp", wp, ho)
-                mx(p1[:, 128:256], lc, ls, WP, 128, True, True)
-                mx(p2[:, 384:512], lc, ls, WP + 128, 128, True, True)
+                mx(pm[:, 128:256], lc, ls, WP, 128, True, True)
                 mx(s2[:], lc, ls, WP, 256, False, False)
                 lc, ls = lhs("hm", wp, ho)
-                mx(p2[:, 0:128], lc, ls, HM, 128, True, True)
-                mx(p1[:, 256:384], lc, ls, HM + 128, 128, True, True)
+                mx(pm[:, 256:384], lc, ls, HM + 128, 128, True, True)
+                lc, ls = lhs("hp", wp, ho)
+                mx(pm[:, 384:512], lc, ls, HP + 128, 128, True, True)
+                nc.vector.tensor_tensor(out=st[:, ho, :], in0=pm[:], in1=bias[:, 0:512], op=ADD)
+            store(0, wp, st)
+            st = stage.tile([P, NHO, 512], F32, tag="st")
+            for ho in range(NHO):
+                last = wp == 7 and ho == NHO - 1
+                pm = mmp.tile([P, 512], F32, tag="mm")
+                lc, ls = lhs("hm", wp, ho)
+                mx(pm[:, 0:128], lc, ls, HM, 128, True, True)
                 mx(s1[:], lc, ls, HM, 256, False, last)
                 lc, ls = lhs("hp", wp, ho)
-                mx(p2[:, 128:256], lc, ls, HP, 128, True, True)
-                mx(p1[:, 384:512], lc, ls, HP + 128, 128, True, True)
+                mx(pm[:, 128:256], lc, ls, HP, 128, True, True)
                 mx(s2[:], lc, ls, HP, 256, False, last)
-                if ho < GS:
-                    nc.scalar.copy(
-                        out=st3[:, ho, :].rearrange("p (a b c) -> p a b c", a=2, b=2),
-                        in_=p3[:].rearrange("p (a b c) -> p b a c", a=2, b=2),
-                    )
-                else:
-                    nc.vector.tensor_tensor(
-                        out=st3[:, ho, :].rearrange("p (a b c) -> p a b c", a=2, b=2),
-                        in0=p3[:].rearrange("p (a b c) -> p b a c", a=2, b=2),
-                        in1=bias[:, 1024:1536].rearrange("p (a b c) -> p a b c", a=2, b=2),
-                        op=ADD,
-                    )
-                nc.vector.tensor_tensor(out=st1[:, ho, :], in0=p1[:], in1=bias[:, 0:512], op=ADD)
-                nc.vector.tensor_tensor(out=st2[:, ho, :], in0=p2[:], in1=bias[:, 512:1024], op=ADD)
-            if GS > 0:
-                nc.gpsimd.tensor_tensor(
-                    out=st3[:, 0:GS, :],
-                    in0=st3[:, 0:GS, :],
-                    in1=bias[:, 1024:1536].unsqueeze(1).to_broadcast([P, GS, 512]),
-                    op=ADD,
-                )
-            for k, st in enumerate([st1, st2, st3]):
-                nc.sync.dma_start(
-                    out=outs[k][:, 2 * wp : 2 * wp + 2, :, :].rearrange("b w (i o) c -> (w i) b (o c)", o=NHO),
-                    in_=st[:].rearrange("p o c -> p (o c)"),
-                )
+                lc, ls = lhs("wm", wp, ho)
+                mx(pm[:, 256:384], lc, ls, WM + 128, 128, True, True)
+                lc, ls = lhs("wp", wp, ho)
+                mx(pm[:, 384:512], lc, ls, WP + 128, 128, True, True)
+                nc.vector.tensor_tensor(out=st[:, ho, :], in0=pm[:], in1=bias[:, 512:1024], op=ADD)
+            store(1, wp, st)
 
         ssb = const.tile([P, 512], F32)
         ssv = ssb[:].rearrange("p (a b c) -> p b a c", a=2, b=2)

@@ -29,7 +29,7 @@ def tile_modelnew_pa_t_kernel(tc, x, w1, b1, out_0, out_1, out_2, out_3):
     with tc.tile_pool(name="const", bufs=1) as const, tc.tile_pool(name="wpool", bufs=1) as wpool, tc.tile_pool(
         name="xpool", bufs=1
     ) as xpool, tc.tile_pool(name="stage", bufs=NSTAGE) as stage, tc.psum_pool(name="acc", bufs=1) as accp, tc.psum_pool(
-        name="mm", bufs=6
+        name="mm", bufs=7
     ) as mmp:
         brow = const.tile([P, 1536], BF16)
         nc.gpsimd.memset(brow[:], 0.0)
@@ -155,8 +155,7 @@ def tile_modelnew_pa_t_kernel(tc, x, w1, b1, out_0, out_1, out_2, out_3):
                 stop=stop,
             )
 
-        s1 = accp.tile([P, 256], F32)
-        s2 = accp.tile([P, 256], F32)
+        ssum = accp.tile([P, 512], F32)
 
         def store(kk, wp, st):
             nc.sync.dma_start(
@@ -173,56 +172,62 @@ def tile_modelnew_pa_t_kernel(tc, x, w1, b1, out_0, out_1, out_2, out_3):
             if wp % 2 == 1 and wp < 7:
                 quantise_halo((wp + 1) // 2)
                 quantise_chunk((wp + 3) // 2)
-            st = stage.tile([P, NHO, 512], F32, tag="st")
+            st1 = stage.tile([P, NHO, 512], F32, tag="st")
+            st2 = stage.tile([P, NHO, 512], F32, tag="st")
+            for ho in range(NHO):
+                first = wp == 0 and ho == 0
+                pw = mmp.tile([P, 512], F32, tag="mm")
+                ph = mmp.tile([P, 512], F32, tag="mm")
+                if first:
+                    lc, ls = lhs("z", wp, ho)
+                    mx(ssum[:], lc, ls, ZZ, 512, True, False)
+                lc, ls = lhs("wm", wp, ho)
+                mx(pw[:, 0:256], lc, ls, WM, 256, True, True)
+                mx(ssum[:, 0:256], lc, ls, WM, 256, False, False)
+                lc, ls = lhs("wp", wp, ho)
+                mx(pw[:, 256:512], lc, ls, WP, 256, True, True)
+                mx(ssum[:, 256:512], lc, ls, WP, 256, False, False)
+                lc, ls = lhs("hm", wp, ho)
+                mx(ph[:, 0:256], lc, ls, HM, 256, True, True)
+                mx(ssum[:, 0:256], lc, ls, HM, 256, False, False)
+                lc, ls = lhs("hp", wp, ho)
+                mx(ph[:, 256:512], lc, ls, HP, 256, True, True)
+                mx(ssum[:, 256:512], lc, ls, HP, 256, False, False)
+                pwv = pw[:].rearrange("p (i j c) -> p j i c", i=2, j=2)
+                phv = ph[:].rearrange("p (i j c) -> p j i c", i=2, j=2)
+                for (dst, lo, srcv, blo) in (
+                    (st1, 0, pwv[:, 0], 0),
+                    (st2, 256, pwv[:, 1], 768),
+                    (st2, 0, phv[:, 0], 512),
+                    (st1, 256, phv[:, 1], 256),
+                ):
+                    nc.vector.tensor_tensor(
+                        out=dst[:, ho, lo : lo + 256].rearrange("p (i c) -> p i c", i=2),
+                        in0=srcv,
+                        in1=bias[:, blo : blo + 256].rearrange("p (i c) -> p i c", i=2),
+                        op=ADD,
+                    )
+            store(0, wp, st1)
+            store(1, wp, st2)
+            st3 = stage.tile([P, NHO, 512], F32, tag="st")
             for ho in range(NHO):
                 pm = mmp.tile([P, 512], F32, tag="mm")
                 lc, ls = lhs("z", wp, ho)
-                first = wp == 0 and ho == 0
                 mx(pm[:], lc, ls, ZZ, 512, True, True)
-                mx(s1[:], lc, ls, ZZ, 256, first, False)
-                mx(s2[:], lc, ls, ZZ + 256, 256, first, False)
+                if not (wp == 0 and ho == 0):
+                    mx(ssum[:], lc, ls, ZZ, 512, False, wp == 7 and ho == NHO - 1)
                 nc.scalar.copy(
-                    out=st[:, ho, :].rearrange("p (a b c) -> p a b c", a=2, b=2),
+                    out=st3[:, ho, :].rearrange("p (a b c) -> p a b c", a=2, b=2),
                     in_=pm[:].rearrange("p (a b c) -> p b a c", a=2, b=2),
                 )
-                nc.gpsimd.tensor_tensor(out=st[:, ho, :], in0=st[:, ho, :], in1=bias[:, 1024:1536], op=ADD)
-            store(2, wp, st)
-            st = stage.tile([P, NHO, 512], F32, tag="st")
-            for ho in range(NHO):
-                pm = mmp.tile([P, 512], F32, tag="mm")
-                lc, ls = lhs("wm", wp, ho)
-                mx(pm[:, 0:128], lc, ls, WM, 128, True, True)
-                mx(s1[:], lc, ls, WM, 256, False, False)
-                lc, ls = lhs("wp", wp, ho)
-                mx(pm[:, 128:256], lc, ls, WP, 128, True, True)
-                mx(s2[:], lc, ls, WP, 256, False, False)
-                lc, ls = lhs("hm", wp, ho)
-                mx(pm[:, 256:384], lc, ls, HM + 128, 128, True, True)
-                lc, ls = lhs("hp", wp, ho)
-                mx(pm[:, 384:512], lc, ls, HP + 128, 128, True, True)
-                nc.vector.tensor_tensor(out=st[:, ho, :], in0=pm[:], in1=bias[:, 0:512], op=ADD)
-            store(0, wp, st)
-            st = stage.tile([P, NHO, 512], F32, tag="st")
-            for ho in range(NHO):
-                last = wp == 7 and ho == NHO - 1
-                pm = mmp.tile([P, 512], F32, tag="mm")
-                lc, ls = lhs("hm", wp, ho)
-                mx(pm[:, 0:128], lc, ls, HM, 128, True, True)
-                mx(s1[:], lc, ls, HM, 256, False, last)
-                lc, ls = lhs("hp", wp, ho)
-                mx(pm[:, 128:256], lc, ls, HP, 128, True, True)
-                mx(s2[:], lc, ls, HP, 256, False, last)
-                lc, ls = lhs("wm", wp, ho)
-                mx(pm[:, 256:384], lc, ls, WM + 128, 128, True, True)
-                lc, ls = lhs("wp", wp, ho)
-                mx(pm[:, 384:512], lc, ls, WP + 128, 128, True, True)
-                nc.vector.tensor_tensor(out=st[:, ho, :], in0=pm[:], in1=bias[:, 512:1024], op=ADD)
-            store(1, wp, st)
+                nc.gpsimd.tensor_tensor(out=st3[:, ho, :], in0=st3[:, ho, :], in1=bias[:, 1024:1536], op=ADD)
+            store(2, wp, st3)
 
         ssb = const.tile([P, 512], F32)
-        ssv = ssb[:].rearrange("p (a b c) -> p b a c", a=2, b=2)
-        nc.vector.tensor_copy(out=ssv[:, 0], in_=s1[:].rearrange("p (a c) -> p a c", a=2))
-        nc.scalar.copy(out=ssv[:, 1], in_=s2[:].rearrange("p (a c) -> p a c", a=2))
+        nc.vector.tensor_copy(
+            out=ssb[:].rearrange("p (a b c) -> p a b c", a=2, b=2),
+            in_=ssum[:].rearrange("p (a b c) -> p b a c", a=2, b=2),
+        )
         pa = mmp.tile([P, 512], F32, tag="mm")
         nc.tensor.matmul(pa[:], lhsT=ind[:], rhs=ssb[:], start=True, stop=True)
         a_sb = const.tile([P, 512], F32)

@@ -8,16 +8,14 @@ U32 = mybir.dt.uint32
 U8 = mybir.dt.uint8
 ADD = mybir.AluOpType.add
 MULT = mybir.AluOpType.mult
-AX = mybir.AxisListType.X
 
 P = 128
 FLOPS = 2 * 4096 * 512 * 1536
 
+NB = 8
 NHO = 4
-SLOT = 64
-PLANE = 18 * SLOT
-NSTAGE = 8
-CV = 88
+MARGIN = 16
+NSTAGE = 10
 
 ROFPOS = [0, 6, 4, 2, 1, 7, 5, 3, 8, 10, 9, 11]
 WM, HM, WP, HP, ZZ = 0, 256, 512, 768, 1024
@@ -28,8 +26,10 @@ def tile_modelnew_pa_t_kernel(tc, x, w1, b1, out_0, out_1, out_2, out_3):
     outs = [out_0, out_1, out_2]
     with tc.tile_pool(name="const", bufs=1) as const, tc.tile_pool(name="wpool", bufs=1) as wpool, tc.tile_pool(
         name="xpool", bufs=1
-    ) as xpool, tc.tile_pool(name="stage", bufs=NSTAGE) as stage, tc.psum_pool(name="acc", bufs=1) as accp, tc.psum_pool(
-        name="mm", bufs=7
+    ) as xpool, tc.tile_pool(name="gpool", bufs=3) as gpool, tc.tile_pool(name="sums", bufs=2) as sums, tc.tile_pool(
+        name="stage", bufs=NSTAGE
+    ) as stage, tc.psum_pool(name="acc", bufs=2) as accp, tc.psum_pool(name="pap", bufs=1) as pap, tc.psum_pool(
+        name="mm", bufs=5
     ) as mmp:
         brow = const.tile([P, 1536], BF16)
         nc.gpsimd.memset(brow[:], 0.0)
@@ -40,17 +40,22 @@ def tile_modelnew_pa_t_kernel(tc, x, w1, b1, out_0, out_1, out_2, out_3):
                 out=w_sb[:, i * 2048 : (i + 1) * 2048].rearrange("p (r k) -> p r k", k=512),
                 in_=w1[i * 512 : (i + 1) * 512, :].rearrange("(r p) k -> p r k", p=P),
             )
-        raw = xpool.tile([P, 8, 2048], BF16)
-        for b in range(8):
-            nc.sync.dma_start(out=raw[:, b, :], in_=x[b].rearrange("(p j) w h -> p (j w h)", j=4))
+        raw = xpool.tile([P, NB, 2048 + 2 * MARGIN], BF16)
+        nc.gpsimd.memset(raw[:, :, 0:MARGIN], 0.0)
+        nc.gpsimd.memset(raw[:, :, MARGIN + 2048 :], 0.0)
+        for b in range(NB):
+            nc.sync.dma_start(
+                out=raw[:, b, MARGIN : MARGIN + 2048], in_=x[b].rearrange("(p j) w h -> p (j w h)", j=4)
+            )
 
         ident = const.tile([P, P], F32)
         make_identity(nc, ident[:])
         ones_bf = const.tile([P, P], BF16)
         nc.vector.memset(ones_bf[:], 1.0)
-        ind = const.tile([P, P], F32)
-        nc.vector.memset(ind[:], 0.0)
-        nc.vector.tensor_reduce(out=ind[:, 0:8], in_=ident[:].rearrange("p (r m) -> p m r", m=8), axis=AX, op=ADD)
+        pick = const.tile([P, NB, P], F32)
+        nc.vector.memset(pick[:], 0.0)
+        for b in range(NB):
+            nc.vector.memset(pick[:, b, b : b + 1], 1.0)
 
         bias = const.tile([P, 1536], F32)
         for i in range(3):
@@ -72,171 +77,139 @@ def tile_modelnew_pa_t_kernel(tc, x, w1, b1, out_0, out_1, out_2, out_3):
                 for u in range(2):
                     nc.tensor.transpose(pt[:, rr, u, :], w32[:, ROFPOS[2 * i + rr], u, :], ident[:])
             src = pt[:].rearrange("p r u o -> p r o u")
-            if i % 2 == 0:
-                nc.vector.tensor_copy(out=gw32[:, i], in_=src)
-            else:
+            if i < 3:
                 nc.scalar.copy(out=gw32[:, i], in_=src)
-        for i in range(3):
-            nc.vector.quantize_mx(
-                out=wcodes[:, i * 512 : (i + 1) * 512].bitcast(FP8X4),
-                scales=wscales[:, i * 512 : (i + 1) * 512],
-                in_=gw[:, i * 2048 : (i + 1) * 2048],
-            )
-
-        gx = xpool.tile([P, NHO, PLANE, 4], BF16, align_bytes=64)
-        gxb = gx[:, :, SLOT : SLOT + 1024, :].rearrange("p o (c b) j -> p b o c j", b=8)
-        for b in range(8):
-            src = raw[:, b, :].rearrange("p (j c o) -> p o c j", j=4, o=NHO)
-            nc.vector.tensor_copy(out=gxb[:, b, :, 0:CV], in_=src[:, :, 0:CV])
-            nc.scalar.copy(out=gxb[:, b, :, CV:P], in_=src[:, :, CV:P])
-        nc.vector.tensor_copy(out=gx[:, :, 0:SLOT, :], in_=gx[:, :, SLOT : 2 * SLOT, :])
-        nc.scalar.copy(out=gx[:, :, 17 * SLOT : 18 * SLOT, :], in_=gx[:, :, 16 * SLOT : 17 * SLOT, :])
-        hx = xpool.tile([P, 4, 2, 256, 4], BF16, align_bytes=64)
-        g0 = gx[:, 0, SLOT : SLOT + 1024, :].rearrange("p (q v r) j -> p q v (r j)", q=4, v=4)
-        g3 = gx[:, 3, SLOT : SLOT + 1024, :].rearrange("p (q v r) j -> p q v (r j)", q=4, v=4)
-        hm = hx[:, :, 0].rearrange("p q (v r) j -> p q v (r j)", v=4)
-        hp = hx[:, :, 1].rearrange("p q (v r) j -> p q v (r j)", v=4)
-
-        def halo_copies(q0, q1):
-            nc.vector.tensor_copy(out=hm[:, q0:q1, :, 32:256], in_=g3[:, q0:q1, :, 0:224])
-            nc.vector.tensor_copy(out=hm[:, q0:q1, :, 0:32], in_=g0[:, q0:q1, :, 0:32])
-            nc.vector.tensor_copy(out=hp[:, q0:q1, :, 0:224], in_=g0[:, q0:q1, :, 32:256])
-            nc.vector.tensor_copy(out=hp[:, q0:q1, :, 224:256], in_=g3[:, q0:q1, :, 224:256])
-
-        xcodes = xpool.tile([P, NHO, PLANE], U32, align_bytes=64)
-        xscales = xpool.tile([P, NHO, PLANE], U8, align_bytes=64)
-        hcodes = xpool.tile([P, 4, 512], U32, align_bytes=64)
-        hscales = xpool.tile([P, 4, 512], U8, align_bytes=64)
-
-        def quantise_chunk(q):
-            lo = q * 256
-            hi = min(lo + 256, PLANE)
-            for ho in range(NHO):
+            else:
+                nc.vector.tensor_copy(out=gw32[:, i], in_=src)
+            if i % 2 == 1:
+                h = i // 2
                 nc.vector.quantize_mx(
-                    out=xcodes[:, ho, lo:hi].bitcast(FP8X4),
-                    scales=xscales[:, ho, lo:hi],
-                    in_=gx[:, ho, lo:hi, :].rearrange("p c j -> p (c j)"),
+                    out=wcodes[:, h * 512 : (h + 1) * 512].bitcast(FP8X4),
+                    scales=wscales[:, h * 512 : (h + 1) * 512],
+                    in_=gw[:, h * 2048 : (h + 1) * 2048],
                 )
 
-        def quantise_halo(q):
-            nc.vector.quantize_mx(
-                out=hcodes[:, q, :].bitcast(FP8X4),
-                scales=hscales[:, q, :],
-                in_=hx[:, q].rearrange("p s c j -> p (s c j)"),
+        def regroup(b):
+            g = gpool.tile([P, 6, 144, 4], BF16, align_bytes=64, tag="g")
+            lo = MARGIN - 1
+            nc.scalar.copy(
+                out=g[:, 0:4, 8:136, :],
+                in_=raw[:, b, lo : lo + 2048].rearrange("p (j c o) -> p o c j", j=4, o=4),
             )
+            other = nc.vector.tensor_copy if b == 0 else nc.scalar.copy
+            other(
+                out=g[:, 4:6, 8:136, :],
+                in_=raw[:, b, lo + 4 : lo + 4 + 2048].rearrange("p (j c o) -> p o c j", j=4, o=4)[:, 0:2],
+            )
+            rows = raw[:, b, MARGIN : MARGIN + 2048].rearrange("p (j w r) -> p w r j", j=4, r=32)
+            nc.scalar.copy(out=g[:, 0, 8:136, :].rearrange("p (w i) j -> p w i j", i=8)[:, :, 0, :], in_=rows[:, :, 0, :])
+            other(out=g[:, 5, 8:136, :].rearrange("p (w i) j -> p w i j", i=8)[:, :, 7, :], in_=rows[:, :, 31, :])
+            other(out=g[:, 1:5, 0:8, :], in_=g[:, 1:5, 8:16, :])
+            other(out=g[:, 1:5, 136:144, :], in_=g[:, 1:5, 128:136, :])
+            return g
 
-        def lhs(kind, wp, ho):
-            o0 = (2 * wp + 1) * SLOT
-            if kind == "wm":
-                return xcodes[:, ho, o0 - SLOT : o0 + SLOT], xscales[:, ho, o0 - SLOT : o0 + SLOT]
-            if kind == "wp":
-                return xcodes[:, ho, o0 + SLOT : o0 + 3 * SLOT], xscales[:, ho, o0 + SLOT : o0 + 3 * SLOT]
-            if kind == "hm" and ho == 0:
-                c0 = (wp % 2) * P
-                return hcodes[:, wp // 2, c0 : c0 + P], hscales[:, wp // 2, c0 : c0 + P]
-            if kind == "hp" and ho == NHO - 1:
-                c0 = 256 + (wp % 2) * P
-                return hcodes[:, wp // 2, c0 : c0 + P], hscales[:, wp // 2, c0 : c0 + P]
-            pl = ho
-            if kind == "hm":
-                pl = ho - 1
-            if kind == "hp":
-                pl = ho + 1
-            return xcodes[:, pl, o0 : o0 + P], xscales[:, pl, o0 : o0 + P]
+        def quantise(g):
+            xc = gpool.tile([P, 14, P], U32, align_bytes=64, tag="xc")
+            xs = gpool.tile([P, 14, P], U8, align_bytes=64, tag="xs")
 
-        def mx(out, lc, ls, col, n, start, stop):
+            def one(idx, q, c0):
+                nc.vector.quantize_mx(
+                    out=xc[:, idx, :].bitcast(FP8X4),
+                    scales=xs[:, idx, :],
+                    in_=g[:, q, c0 : c0 + P, :].rearrange("p c j -> p (c j)"),
+                )
+
+            one(1, 1, 8)
+            one(0, 0, 8)
+            for ho in range(NHO):
+                one(6 + ho, ho + 1, 0)
+                one(10 + ho, ho + 1, 16)
+                one(ho + 2, ho + 2, 8)
+            return xc, xs
+
+        def mx(out, xcs, idx, col, n, start, stop):
             nc.tensor.matmul_mx(
                 out=out,
-                lhsT=lc.bitcast(FP8X4),
-                lhsT_scale=ls,
+                lhsT=xcs[0][:, idx, :].bitcast(FP8X4),
+                lhsT_scale=xcs[1][:, idx, :],
                 rhs=wcodes[:, col : col + n].bitcast(FP8X4),
                 rhs_scale=wscales[:, col : col + n],
                 start=start,
                 stop=stop,
             )
 
-        ssum = accp.tile([P, 512], F32)
-
-        def store(kk, wp, st):
+        def store(kk, b, st):
             nc.sync.dma_start(
-                out=outs[kk][:, 2 * wp : 2 * wp + 2, :, :].rearrange("b w (i o) c -> (w i) b (o c)", o=NHO),
+                out=outs[kk][b].rearrange("w (i o) c -> (w i) (o c)", o=NHO),
                 in_=st[:].rearrange("p o c -> p (o c)"),
             )
 
-        quantise_chunk(0)
-        halo_copies(0, 1)
-        quantise_halo(0)
-        quantise_chunk(1)
-        halo_copies(1, 4)
-        for wp in range(8):
-            if wp % 2 == 1 and wp < 7:
-                quantise_halo((wp + 1) // 2)
-                quantise_chunk((wp + 3) // 2)
-            st1 = stage.tile([P, NHO, 512], F32, tag="st")
-            st2 = stage.tile([P, NHO, 512], F32, tag="st")
-            for ho in range(NHO):
-                first = wp == 0 and ho == 0
-                pw = mmp.tile([P, 512], F32, tag="mm")
-                ph = mmp.tile([P, 512], F32, tag="mm")
-                if first:
-                    lc, ls = lhs("z", wp, ho)
-                    mx(ssum[:], lc, ls, ZZ, 512, True, False)
-                lc, ls = lhs("wm", wp, ho)
-                mx(pw[:, 0:256], lc, ls, WM, 256, True, True)
-                mx(ssum[:, 0:256], lc, ls, WM, 256, False, False)
-                lc, ls = lhs("wp", wp, ho)
-                mx(pw[:, 256:512], lc, ls, WP, 256, True, True)
-                mx(ssum[:, 256:512], lc, ls, WP, 256, False, False)
-                lc, ls = lhs("hm", wp, ho)
-                mx(ph[:, 0:256], lc, ls, HM, 256, True, True)
-                mx(ssum[:, 0:256], lc, ls, HM, 256, False, False)
-                lc, ls = lhs("hp", wp, ho)
-                mx(ph[:, 256:512], lc, ls, HP, 256, True, True)
-                mx(ssum[:, 256:512], lc, ls, HP, 256, False, False)
-                pwv = pw[:].rearrange("p (i j c) -> p j i c", i=2, j=2)
-                phv = ph[:].rearrange("p (i j c) -> p j i c", i=2, j=2)
-                for (dst, lo, srcv, blo) in (
-                    (st1, 0, pwv[:, 0], 0),
-                    (st2, 256, pwv[:, 1], 768),
-                    (st2, 0, phv[:, 0], 512),
-                    (st1, 256, phv[:, 1], 256),
-                ):
-                    nc.vector.tensor_tensor(
-                        out=dst[:, ho, lo : lo + 256].rearrange("p (i c) -> p i c", i=2),
-                        in0=srcv,
-                        in1=bias[:, blo : blo + 256].rearrange("p (i c) -> p i c", i=2),
-                        op=ADD,
-                    )
-            store(0, wp, st1)
-            store(1, wp, st2)
-            st3 = stage.tile([P, NHO, 512], F32, tag="st")
+        pa = pap.tile([P, 512], F32)
+
+        def add_partitions(b, ssb):
+            nc.tensor.matmul(pa[:], lhsT=pick[:, b, :], rhs=ssb[:], start=(b == 0), stop=(b == NB - 1))
+
+        codes = quantise(regroup(0))
+        ssb_prev = None
+        for b in range(NB):
+            if b + 1 < NB:
+                g_next = regroup(b + 1)
+            ssum = accp.tile([P, 512], F32, tag="ss")
+            mx(ssum[:], codes, 1, ZZ, 512, True, False)
+            st = stage.tile([P, NHO, 512], F32, tag="st")
             for ho in range(NHO):
                 pm = mmp.tile([P, 512], F32, tag="mm")
-                lc, ls = lhs("z", wp, ho)
-                mx(pm[:], lc, ls, ZZ, 512, True, True)
-                if not (wp == 0 and ho == 0):
-                    mx(ssum[:], lc, ls, ZZ, 512, False, wp == 7 and ho == NHO - 1)
-                nc.scalar.copy(
-                    out=st3[:, ho, :].rearrange("p (a b c) -> p a b c", a=2, b=2),
-                    in_=pm[:].rearrange("p (a b c) -> p b a c", a=2, b=2),
-                )
-                nc.gpsimd.tensor_tensor(out=st3[:, ho, :], in0=st3[:, ho, :], in1=bias[:, 1024:1536], op=ADD)
-            store(2, wp, st3)
+                mx(pm[:, 0:128], codes, 6 + ho, WM, 128, True, True)
+                mx(ssum[:, 0:256], codes, 6 + ho, WM, 256, False, False)
+                mx(pm[:, 128:256], codes, 10 + ho, WP, 128, True, True)
+                mx(ssum[:, 256:512], codes, 10 + ho, WP, 256, False, False)
+                mx(pm[:, 256:384], codes, ho, HM + 128, 128, True, True)
+                mx(pm[:, 384:512], codes, ho + 2, HP + 128, 128, True, True)
+                nc.vector.tensor_tensor(out=st[:, ho, :], in0=pm[:], in1=bias[:, 0:512], op=ADD)
+            store(0, b, st)
+            if b > 0:
+                add_partitions(b - 1, ssb_prev)
+            st = stage.tile([P, NHO, 512], F32, tag="st")
+            for ho in range(NHO):
+                pm = mmp.tile([P, 512], F32, tag="mm")
+                mx(pm[:, 0:128], codes, ho, HM, 128, True, True)
+                mx(ssum[:, 0:256], codes, ho, HM, 256, False, False)
+                mx(pm[:, 128:256], codes, ho + 2, HP, 128, True, True)
+                mx(ssum[:, 256:512], codes, ho + 2, HP, 256, False, False)
+                mx(pm[:, 256:384], codes, 6 + ho, WM + 128, 128, True, True)
+                mx(pm[:, 384:512], codes, 10 + ho, WP + 128, 128, True, True)
+                nc.vector.tensor_tensor(out=st[:, ho, :], in0=pm[:], in1=bias[:, 512:1024], op=ADD)
+            store(1, b, st)
+            if b + 1 < NB:
+                codes_next = quantise(g_next)
+            st = stage.tile([P, NHO, 512], F32, tag="st")
+            for ho in range(NHO):
+                pm = mmp.tile([P, 512], F32, tag="mm")
+                mx(pm[:], codes, ho + 1, ZZ, 512, True, True)
+                if ho > 0:
+                    mx(ssum[:], codes, ho + 1, ZZ, 512, False, ho == NHO - 1)
+                natural = st[:, ho, :].rearrange("p (a b c) -> p a b c", a=2, b=2)
+                swapped = pm[:].rearrange("p (a b c) -> p b a c", a=2, b=2)
+                if b + 1 < NB:
+                    nc.scalar.copy(out=natural, in_=swapped)
+                    nc.gpsimd.tensor_tensor(out=st[:, ho, :], in0=st[:, ho, :], in1=bias[:, 1024:1536], op=ADD)
+                else:
+                    nc.vector.tensor_tensor(
+                        out=natural,
+                        in0=swapped,
+                        in1=bias[:, 1024:1536].rearrange("p (a b c) -> p a b c", a=2, b=2),
+                        op=ADD,
+                    )
+            store(2, b, st)
+            ssb_prev = sums.tile([P, 512], F32, tag="ssb")
+            nc.scalar.copy(
+                out=ssb_prev[:].rearrange("p (a b c) -> p a b c", a=2, b=2),
+                in_=ssum[:].rearrange("p (a b c) -> p b a c", a=2, b=2),
+            )
+            if b + 1 < NB:
+                codes = codes_next
 
-        ssb = const.tile([P, 512], F32)
-        nc.vector.tensor_copy(
-            out=ssb[:].rearrange("p (a b c) -> p a b c", a=2, b=2),
-            in_=ssum[:].rearrange("p (a b c) -> p b a c", a=2, b=2),
-        )
-        pa = mmp.tile([P, 512], F32, tag="mm")
-        nc.tensor.matmul(pa[:], lhsT=ind[:], rhs=ssb[:], start=True, stop=True)
+        add_partitions(NB - 1, ssb_prev)
         a_sb = const.tile([P, 512], F32)
-        nc.vector.scalar_tensor_tensor(
-            out=a_sb[:],
-            in0=bsum[:],
-            scalar=512.0,
-            in1=pa[:],
-            op0=MULT,
-            op1=ADD,
-        )
+        nc.vector.scalar_tensor_tensor(out=a_sb[:], in0=bsum[:], scalar=512.0, in1=pa[:], op0=MULT, op1=ADD)
         nc.sync.dma_start(out=out_3, in_=a_sb[0:8, :])

@@ -6,6 +6,7 @@ BF16 = mybir.dt.bfloat16
 F32 = mybir.dt.float32
 U32 = mybir.dt.uint32
 U8 = mybir.dt.uint8
+I32 = mybir.dt.int32
 ADD = mybir.AluOpType.add
 MULT = mybir.AluOpType.mult
 
@@ -15,6 +16,7 @@ FLOPS = 2 * 4096 * 512 * 1536
 NB = 8
 NHO = 4
 MARGIN = 16
+LEAD = 48
 NSTAGE = 10
 
 ROFPOS = [0, 6, 4, 2, 1, 7, 5, 3, 8, 10, 9, 11]
@@ -69,8 +71,10 @@ def tile_modelnew_pa_t_kernel(tc, x, w1, b1, out_0, out_1, out_2, out_3):
         w32 = w_sb[:].bitcast(F32).rearrange("p (r q u) -> p r u q", r=12, u=2)
         gw = wpool.tile([P, 6144], BF16, align_bytes=64)
         gw32 = gw[:].bitcast(F32).rearrange("p (i r o u) -> p i r o u", i=6, r=2, u=2)
-        wcodes = wpool.tile([P, 1536], U32, align_bytes=64)
-        wscales = wpool.tile([P, 1536], U8, align_bytes=64)
+        wcodes = wpool.tile([P, 1536], U32, align_bytes=256)
+        wscales = wpool.tile([P, 1536], U8, align_bytes=256)
+        wslots = wpool.tile([P, 12, 256], U8, align_bytes=256)
+        nc.vector.memset(wscales[:].bitcast(I32), 0)
         for i in range(6):
             pt = mmp.tile([P, 2, 2, P], F32, tag="mm")
             for rr in range(2):
@@ -88,6 +92,10 @@ def tile_modelnew_pa_t_kernel(tc, x, w1, b1, out_0, out_1, out_2, out_3):
                     scales=wscales[:, h * 512 : (h + 1) * 512],
                     in_=gw[:, h * 2048 : (h + 1) * 2048],
                 )
+
+        nc.vector.tensor_copy(
+            out=wslots[:, :, 0:128].bitcast(I32), in_=wscales[:].bitcast(I32).rearrange("p (t c) -> p t c", t=12)
+        )
 
         def regroup(b):
             g = gpool.tile([P, 6, 144, 4], BF16, align_bytes=64, tag="g")
@@ -109,13 +117,13 @@ def tile_modelnew_pa_t_kernel(tc, x, w1, b1, out_0, out_1, out_2, out_3):
             return g
 
         def quantise(g):
-            xc = gpool.tile([P, 14, P], U32, align_bytes=64, tag="xc")
-            xs = gpool.tile([P, 14, P], U8, align_bytes=64, tag="xs")
+            xc = gpool.tile([P, LEAD + 14 * P], U32, align_bytes=256, tag="xc")
+            xs = gpool.tile([P, 14, 256], U8, align_bytes=256, tag="xs")
 
             def one(idx, q, c0):
                 nc.vector.quantize_mx(
-                    out=xc[:, idx, :].bitcast(FP8X4),
-                    scales=xs[:, idx, :],
+                    out=xc[:, LEAD + idx * P : LEAD + (idx + 1) * P].bitcast(FP8X4),
+                    scales=xs[:, idx, 0:P],
                     in_=g[:, q, c0 : c0 + P, :].rearrange("p c j -> p (c j)"),
                 )
 
@@ -130,10 +138,10 @@ def tile_modelnew_pa_t_kernel(tc, x, w1, b1, out_0, out_1, out_2, out_3):
         def mx(out, xcs, idx, col, n, start, stop):
             nc.tensor.matmul_mx(
                 out=out,
-                lhsT=xcs[0][:, idx, :].bitcast(FP8X4),
-                lhsT_scale=xcs[1][:, idx, :],
+                lhsT=xcs[0][:, LEAD + idx * P : LEAD + (idx + 1) * P].bitcast(FP8X4),
+                lhsT_scale=xcs[1][:, idx, 0:P],
                 rhs=wcodes[:, col : col + n].bitcast(FP8X4),
-                rhs_scale=wscales[:, col : col + n],
+                rhs_scale=wslots[:, col // P, 0:P] if n == P else wscales[:, col : col + n],
                 start=start,
                 stop=stop,
             )

@@ -14,10 +14,10 @@ P = 128
 FLOPS = 2 * 4096 * 512 * 1536
 
 NB = 8
-NHO = 4
-MARGIN = 16
-LEAD = 48
+NG = 2
 NSTAGE = 10
+
+QM, QP, PM, PP = 16, 20, 24, 28
 
 ROFPOS = [0, 6, 4, 2, 1, 7, 5, 3, 8, 10, 9, 11]
 WM, HM, WP, HP, ZZ = 0, 256, 512, 768, 1024
@@ -28,63 +28,118 @@ def tile_modelnew_pa_t_kernel(tc, x, w1, b1, out_0, out_1, out_2, out_3):
     outs = [out_0, out_1, out_2]
     with tc.tile_pool(name="const", bufs=1) as const, tc.tile_pool(name="wpool", bufs=1) as wpool, tc.tile_pool(
         name="xpool", bufs=1
-    ) as xpool, tc.tile_pool(name="gpool", bufs=3) as gpool, tc.tile_pool(name="sums", bufs=2) as sums, tc.tile_pool(
-        name="stage", bufs=NSTAGE
-    ) as stage, tc.psum_pool(name="acc", bufs=2) as accp, tc.psum_pool(name="pap", bufs=1) as pap, tc.psum_pool(
-        name="mm", bufs=5
-    ) as mmp:
+    ) as xpool, tc.tile_pool(name="gpool", bufs=1) as gpool, tc.tile_pool(name="cpool", bufs=2) as cpool, tc.tile_pool(
+        name="sums", bufs=2
+    ) as sums, tc.tile_pool(name="stage", bufs=NSTAGE) as stage, tc.psum_pool(name="acc", bufs=2) as accp, tc.psum_pool(
+        name="pap", bufs=1
+    ) as pap, tc.psum_pool(name="mm", bufs=5) as mmp:
         brow = const.tile([P, 1536], BF16)
         nc.gpsimd.memset(brow[:], 0.0)
         nc.sync.dma_start(out=brow[0:1, :], in_=b1.unsqueeze(0))
+        raw = xpool.tile([P, NB, 2048], BF16)
         w_sb = wpool.tile([P, 12 * 512], BF16)
+
+        def load_x(b):
+            nc.sync.dma_start(out=raw[:, b, :], in_=x[b].rearrange("(p j) w h -> p (j w h)", j=4))
+
+        for b in range(4):
+            load_x(b)
         for i in range(3):
             nc.sync.dma_start(
                 out=w_sb[:, i * 2048 : (i + 1) * 2048].rearrange("p (r k) -> p r k", k=512),
                 in_=w1[i * 512 : (i + 1) * 512, :].rearrange("(r p) k -> p r k", p=P),
             )
-        raw = xpool.tile([P, NB, 2048 + 2 * MARGIN], BF16)
-        nc.gpsimd.memset(raw[:, :, 0:MARGIN], 0.0)
-        nc.gpsimd.memset(raw[:, :, MARGIN + 2048 :], 0.0)
-        for b in range(NB):
-            nc.sync.dma_start(
-                out=raw[:, b, MARGIN : MARGIN + 2048], in_=x[b].rearrange("(p j) w h -> p (j w h)", j=4)
-            )
+        for b in range(4, NB):
+            load_x(b)
 
         ident = const.tile([P, P], F32)
         make_identity(nc, ident[:])
         ones_bf = const.tile([P, P], BF16)
         nc.vector.memset(ones_bf[:], 1.0)
-        pick = const.tile([P, NB, P], F32)
-        nc.vector.memset(pick[:], 0.0)
-        for b in range(NB):
-            nc.vector.memset(pick[:, b, b : b + 1], 1.0)
+        pick = const.tile([P, NG, P], F32)
+        nc.gpsimd.memset(pick[:], 0.0)
+        for g in range(NG):
+            for b4 in range(4):
+                nc.gpsimd.memset(pick[32 * b4 : 32 * b4 + 32, g, 4 * g + b4 : 4 * g + b4 + 1], 1.0)
+
+        def regroup(gt, b, copy):
+            b4 = b % 4
+            copy(
+                out=gt[:, :, :, 32 * b4 : 32 * b4 + 32, :].rearrange("p v r (q i) j -> p r q v i j", q=4),
+                in_=raw[:, b, :].rearrange("p (j q v i r) -> p r q v i j", j=4, q=4, v=4, i=8),
+            )
+
+        def new_group():
+            gt = gpool.tile([P, 4, 4, P, 4], BF16, align_bytes=64, tag="g")
+            return gt
+
+        def quantise(gt):
+            xc = cpool.tile([P, 32 * P], U32, align_bytes=64, tag="xc")
+            xs = cpool.tile([P, 32 * P], U8, align_bytes=64, tag="xs")
+            for v in range(4):
+                nc.vector.quantize_mx(
+                    out=xc[:, v * 512 : (v + 1) * 512].bitcast(FP8X4),
+                    scales=xs[:, v * 512 : (v + 1) * 512],
+                    in_=gt[:, v].rearrange("p r m j -> p (r m j)"),
+                )
+            return xc, xs
+
+        def move(flat, i):
+            mv = nc.vector.tensor_copy
+            n = 16 * i
+            bq = flat[:, 0 : 16 * n].rearrange("p (v r b q i) -> p v r b q i", v=4, r=4, b=4, q=4)
+            qm = flat[:, QM * n : (QM + 4) * n].rearrange("p (r b q i) -> p r b q i", r=4, b=4, q=4)
+            qp = flat[:, QP * n : (QP + 4) * n].rearrange("p (r b q i) -> p r b q i", r=4, b=4, q=4)
+            mv(out=qm[:, :, :, 1:4, :], in_=bq[:, 3, :, :, 0:3, :])
+            mv(out=qm[:, :, :, 0, :], in_=bq[:, 0, :, :, 0, :])
+            mv(out=qp[:, :, :, 0:3, :], in_=bq[:, 0, :, :, 1:4, :])
+            mv(out=qp[:, :, :, 3, :], in_=bq[:, 3, :, :, 3, :])
+
+        def move_h(flat):
+            mv = nc.vector.tensor_copy
+            bi = flat[:, 0 : 16 * P].rearrange("p (v r m i) -> p v r m i", v=4, r=4, i=8)
+            pm = flat[:, PM * P : (PM + 4) * P].rearrange("p (v m i) -> p v m i", v=4, i=8)
+            pp = flat[:, PP * P : (PP + 4) * P].rearrange("p (v m i) -> p v m i", v=4, i=8)
+            mv(out=pm[:, :, :, 1:8], in_=bi[:, :, 3, :, 0:7])
+            mv(out=pm[:, :, :, 0], in_=bi[:, :, 0, :, 0])
+            mv(out=pp[:, :, :, 0:7], in_=bi[:, :, 0, :, 1:8])
+            mv(out=pp[:, :, :, 7], in_=bi[:, :, 3, :, 7])
+
+        def moves(xcs):
+            xc, xs = xcs
+            move_h(xc[:].bitcast(I32))
+            move_h(xs[:])
+            move(xc[:].bitcast(I32), 8)
+            move(xs[:].bitcast(I32), 2)
+
+        gt0 = new_group()
+        regroup(gt0, 0, nc.scalar.copy)
+        regroup(gt0, 1, nc.vector.tensor_copy)
+        regroup(gt0, 2, nc.scalar.copy)
+        regroup(gt0, 3, nc.vector.tensor_copy)
+        codes = quantise(gt0)
+        moves(codes)
 
         bias = const.tile([P, 1536], F32)
         for i in range(3):
             pb = mmp.tile([P, 512], F32, tag="mm")
             nc.tensor.matmul(pb[:], lhsT=ones_bf[:], rhs=brow[:, i * 512 : (i + 1) * 512], start=True, stop=True)
-            nc.vector.tensor_copy(out=bias[:, i * 512 : (i + 1) * 512], in_=pb[:])
+            nc.scalar.copy(out=bias[:, i * 512 : (i + 1) * 512], in_=pb[:])
         bsum = const.tile([P, 512], F32)
-        nc.vector.tensor_tensor(out=bsum[:], in0=bias[:, 0:512], in1=bias[:, 512:1024], op=ADD)
-        nc.vector.tensor_tensor(out=bsum[:], in0=bsum[:], in1=bias[:, 1024:1536], op=ADD)
+        nc.gpsimd.tensor_tensor(out=bsum[:], in0=bias[:, 0:512], in1=bias[:, 512:1024], op=ADD)
+        nc.gpsimd.tensor_tensor(out=bsum[:], in0=bsum[:], in1=bias[:, 1024:1536], op=ADD)
 
         w32 = w_sb[:].bitcast(F32).rearrange("p (r q u) -> p r u q", r=12, u=2)
         gw = wpool.tile([P, 6144], BF16, align_bytes=64)
         gw32 = gw[:].bitcast(F32).rearrange("p (i r o u) -> p i r o u", i=6, r=2, u=2)
-        wcodes = wpool.tile([P, 1536], U32, align_bytes=256)
-        wscales = wpool.tile([P, 1536], U8, align_bytes=256)
-        wslots = wpool.tile([P, 12, 256], U8, align_bytes=256)
-        nc.vector.memset(wscales[:].bitcast(I32), 0)
+        wcodes = wpool.tile([P, 1536], U32, align_bytes=64)
+        wscales = wpool.tile([P, 1536], U8, align_bytes=64)
         for i in range(6):
             pt = mmp.tile([P, 2, 2, P], F32, tag="mm")
             for rr in range(2):
                 for u in range(2):
                     nc.tensor.transpose(pt[:, rr, u, :], w32[:, ROFPOS[2 * i + rr], u, :], ident[:])
-            src = pt[:].rearrange("p r u o -> p r o u")
-            if i < 3:
-                nc.scalar.copy(out=gw32[:, i], in_=src)
-            else:
-                nc.vector.tensor_copy(out=gw32[:, i], in_=src)
+            nc.scalar.copy(out=gw32[:, i], in_=pt[:].rearrange("p r u o -> p r o u"))
             if i % 2 == 1:
                 h = i // 2
                 nc.vector.quantize_mx(
@@ -93,131 +148,112 @@ def tile_modelnew_pa_t_kernel(tc, x, w1, b1, out_0, out_1, out_2, out_3):
                     in_=gw[:, h * 2048 : (h + 1) * 2048],
                 )
 
-        nc.vector.tensor_copy(
-            out=wslots[:, :, 0:128].bitcast(I32), in_=wscales[:].bitcast(I32).rearrange("p (t c) -> p t c", t=12)
-        )
-
-        def regroup(b):
-            g = gpool.tile([P, 6, 144, 4], BF16, align_bytes=64, tag="g")
-            lo = MARGIN - 1
-            nc.scalar.copy(
-                out=g[:, 0:4, 8:136, :],
-                in_=raw[:, b, lo : lo + 2048].rearrange("p (j c o) -> p o c j", j=4, o=4),
-            )
-            other = nc.vector.tensor_copy if b == 0 else nc.scalar.copy
-            other(
-                out=g[:, 4:6, 8:136, :],
-                in_=raw[:, b, lo + 4 : lo + 4 + 2048].rearrange("p (j c o) -> p o c j", j=4, o=4)[:, 0:2],
-            )
-            rows = raw[:, b, MARGIN : MARGIN + 2048].rearrange("p (j w r) -> p w r j", j=4, r=32)
-            nc.scalar.copy(out=g[:, 0, 8:136, :].rearrange("p (w i) j -> p w i j", i=8)[:, :, 0, :], in_=rows[:, :, 0, :])
-            other(out=g[:, 5, 8:136, :].rearrange("p (w i) j -> p w i j", i=8)[:, :, 7, :], in_=rows[:, :, 31, :])
-            other(out=g[:, 1:5, 0:8, :], in_=g[:, 1:5, 8:16, :])
-            other(out=g[:, 1:5, 136:144, :], in_=g[:, 1:5, 128:136, :])
-            return g
-
-        def quantise(g):
-            xc = gpool.tile([P, LEAD + 14 * P], U32, align_bytes=256, tag="xc")
-            xs = gpool.tile([P, 14, 256], U8, align_bytes=256, tag="xs")
-
-            def one(idx, q, c0):
-                nc.vector.quantize_mx(
-                    out=xc[:, LEAD + idx * P : LEAD + (idx + 1) * P].bitcast(FP8X4),
-                    scales=xs[:, idx, 0:P],
-                    in_=g[:, q, c0 : c0 + P, :].rearrange("p c j -> p (c j)"),
-                )
-
-            one(1, 1, 8)
-            one(0, 0, 8)
-            for ho in range(NHO):
-                one(6 + ho, ho + 1, 0)
-                one(10 + ho, ho + 1, 16)
-                one(ho + 2, ho + 2, 8)
-            return xc, xs
-
-        def mx(out, xcs, idx, col, n, start, stop):
+        def mx(out, xcs, t, col, n, start, stop):
             nc.tensor.matmul_mx(
                 out=out,
-                lhsT=xcs[0][:, LEAD + idx * P : LEAD + (idx + 1) * P].bitcast(FP8X4),
-                lhsT_scale=xcs[1][:, idx, 0:P],
+                lhsT=xcs[0][:, t * P : (t + 1) * P].bitcast(FP8X4),
+                lhsT_scale=xcs[1][:, t * P : (t + 1) * P],
                 rhs=wcodes[:, col : col + n].bitcast(FP8X4),
-                rhs_scale=wslots[:, col // P, 0:P] if n == P else wscales[:, col : col + n],
+                rhs_scale=wscales[:, col : col + n],
                 start=start,
                 stop=stop,
             )
 
-        def store(kk, b, st):
-            nc.sync.dma_start(
-                out=outs[kk][b].rearrange("w (i o) c -> (w i) (o c)", o=NHO),
-                in_=st[:].rearrange("p o c -> p (o c)"),
-            )
+        def store(k, g, v, st):
+            if k == 1:
+                dst = outs[k][4 * g : 4 * g + 4].rearrange("b (q v) h c -> v (b q) (h c)", v=4)[v]
+            else:
+                dst = outs[k][4 * g : 4 * g + 4].rearrange("b (q v) (i o) c -> v (b q) i (o c)", v=4, o=4)[v]
+            nc.sync.dma_start(out=dst, in_=st[:].rearrange("p o c -> p (o c)"))
 
         pa = pap.tile([P, 512], F32)
 
-        def add_partitions(b, ssb):
-            nc.tensor.matmul(pa[:], lhsT=pick[:, b, :], rhs=ssb[:], start=(b == 0), stop=(b == NB - 1))
+        def add_partitions(g, ssb):
+            nc.tensor.matmul(pa[:], lhsT=pick[:, g, :], rhs=ssb[:], start=(g == 0), stop=(g == NG - 1))
 
-        codes = quantise(regroup(0))
-        ssb_prev = None
-        for b in range(NB):
-            if b + 1 < NB:
-                g_next = regroup(b + 1)
+        SLOTS = [1, 2, 0, 3]
+        ssbs = []
+        for g in range(NG):
             ssum = accp.tile([P, 512], F32, tag="ss")
-            mx(ssum[:], codes, 1, ZZ, 512, True, False)
-            st = stage.tile([P, NHO, 512], F32, tag="st")
-            for ho in range(NHO):
+            mx(ssum[:], codes, SLOTS[0] * 4, ZZ, 512, True, False)
+
+            def bank1(st, v, r):
+                wm = (v - 1) * 4 + r if v > 0 else QM + r
+                wp = (v + 1) * 4 + r if v < 3 else QP + r
+                hm = v * 4 + r - 1 if r > 0 else PM + v
+                hp = v * 4 + r + 1 if r < 3 else PP + v
                 pm = mmp.tile([P, 512], F32, tag="mm")
-                mx(pm[:, 0:128], codes, 6 + ho, WM, 128, True, True)
-                mx(ssum[:, 0:256], codes, 6 + ho, WM, 256, False, False)
-                mx(pm[:, 128:256], codes, 10 + ho, WP, 128, True, True)
-                mx(ssum[:, 256:512], codes, 10 + ho, WP, 256, False, False)
-                mx(pm[:, 256:384], codes, ho, HM + 128, 128, True, True)
-                mx(pm[:, 384:512], codes, ho + 2, HP + 128, 128, True, True)
-                nc.vector.tensor_tensor(out=st[:, ho, :], in0=pm[:], in1=bias[:, 0:512], op=ADD)
-            store(0, b, st)
-            if b > 0:
-                add_partitions(b - 1, ssb_prev)
-            st = stage.tile([P, NHO, 512], F32, tag="st")
-            for ho in range(NHO):
+                mx(pm[:, 0:128], codes, wm, WM, 128, True, True)
+                mx(ssum[:, 0:256], codes, wm, WM, 256, False, False)
+                mx(pm[:, 128:256], codes, wp, WP, 128, True, True)
+                mx(ssum[:, 256:512], codes, wp, WP, 256, False, False)
+                mx(pm[:, 256:384], codes, hm, HM + 128, 128, True, True)
+                mx(pm[:, 384:512], codes, hp, HP + 128, 128, True, True)
+                nc.vector.tensor_tensor(out=st[:, r, :], in0=pm[:], in1=bias[:, 0:512], op=ADD)
+
+            def bank2(st, v, r):
+                wm = (v - 1) * 4 + r if v > 0 else QM + r
+                wp = (v + 1) * 4 + r if v < 3 else QP + r
+                hm = v * 4 + r - 1 if r > 0 else PM + v
+                hp = v * 4 + r + 1 if r < 3 else PP + v
                 pm = mmp.tile([P, 512], F32, tag="mm")
-                mx(pm[:, 0:128], codes, ho, HM, 128, True, True)
-                mx(ssum[:, 0:256], codes, ho, HM, 256, False, False)
-                mx(pm[:, 128:256], codes, ho + 2, HP, 128, True, True)
-                mx(ssum[:, 256:512], codes, ho + 2, HP, 256, False, False)
-                mx(pm[:, 256:384], codes, 6 + ho, WM + 128, 128, True, True)
-                mx(pm[:, 384:512], codes, 10 + ho, WP + 128, 128, True, True)
-                nc.vector.tensor_tensor(out=st[:, ho, :], in0=pm[:], in1=bias[:, 512:1024], op=ADD)
-            store(1, b, st)
-            if b + 1 < NB:
-                codes_next = quantise(g_next)
-            st = stage.tile([P, NHO, 512], F32, tag="st")
-            for ho in range(NHO):
+                mx(pm[:, 0:128], codes, hm, HM, 128, True, True)
+                mx(ssum[:, 0:256], codes, hm, HM, 256, False, False)
+                mx(pm[:, 128:256], codes, hp, HP, 128, True, True)
+                mx(ssum[:, 256:512], codes, hp, HP, 256, False, False)
+                mx(pm[:, 256:384], codes, wm, WM + 128, 128, True, True)
+                mx(pm[:, 384:512], codes, wp, WP + 128, 128, True, True)
+                nc.vector.tensor_tensor(out=st[:, r, :], in0=pm[:], in1=bias[:, 512:1024], op=ADD)
+
+            def bank3(st, v, r, first, last):
                 pm = mmp.tile([P, 512], F32, tag="mm")
-                mx(pm[:], codes, ho + 1, ZZ, 512, True, True)
-                if ho > 0:
-                    mx(ssum[:], codes, ho + 1, ZZ, 512, False, ho == NHO - 1)
-                natural = st[:, ho, :].rearrange("p (a b c) -> p a b c", a=2, b=2)
-                swapped = pm[:].rearrange("p (a b c) -> p b a c", a=2, b=2)
-                if b + 1 < NB:
-                    nc.scalar.copy(out=natural, in_=swapped)
-                    nc.gpsimd.tensor_tensor(out=st[:, ho, :], in0=st[:, ho, :], in1=bias[:, 1024:1536], op=ADD)
-                else:
-                    nc.vector.tensor_tensor(
-                        out=natural,
-                        in0=swapped,
-                        in1=bias[:, 1024:1536].rearrange("p (a b c) -> p a b c", a=2, b=2),
-                        op=ADD,
-                    )
-            store(2, b, st)
-            ssb_prev = sums.tile([P, 512], F32, tag="ssb")
+                mx(pm[:], codes, v * 4 + r, ZZ, 512, True, True)
+                if not first:
+                    mx(ssum[:], codes, v * 4 + r, ZZ, 512, False, last)
+                nc.scalar.copy(
+                    out=st[:, r, :].rearrange("p (a b c) -> p a b c", a=2, b=2),
+                    in_=pm[:].rearrange("p (a b c) -> p b a c", a=2, b=2),
+                )
+                nc.gpsimd.tensor_tensor(out=st[:, r, :], in0=st[:, r, :], in1=bias[:, 1024:1536], op=ADD)
+
+            for n, v in enumerate(SLOTS):
+                st1 = stage.tile([P, 4, 512], F32, tag="st")
+                st3 = stage.tile([P, 4, 512], F32, tag="st")
+                bank1(st1, v, 0)
+                bank3(st3, v, 0, n == 0, False)
+                bank1(st1, v, 1)
+                bank1(st1, v, 2)
+                bank3(st3, v, 1, False, False)
+                bank1(st1, v, 3)
+                store(0, g, v, st1)
+                st2 = stage.tile([P, 4, 512], F32, tag="st")
+                bank2(st2, v, 0)
+                bank3(st3, v, 2, False, False)
+                bank2(st2, v, 1)
+                bank2(st2, v, 2)
+                bank2(st2, v, 3)
+                store(1, g, v, st2)
+                bank3(st3, v, 3, False, n == 3)
+                store(2, g, v, st3)
+                if g + 1 < NG and n == 0:
+                    gt1 = new_group()
+                    for b in range(4, NB):
+                        regroup(gt1, b, nc.scalar.copy)
+                if g + 1 < NG and n == 2:
+                    codes_next = quantise(gt1)
+                    moves(codes_next)
+                if g > 0 and n == 0:
+                    add_partitions(g - 1, ssbs[g - 1])
+            ssb = sums.tile([P, 512], F32, tag="ssb")
             nc.scalar.copy(
-                out=ssb_prev[:].rearrange("p (a b c) -> p a b c", a=2, b=2),
+                out=ssb[:].rearrange("p (a b c) -> p a b c", a=2, b=2),
                 in_=ssum[:].rearrange("p (a b c) -> p b a c", a=2, b=2),
             )
-            if b + 1 < NB:
+            ssbs.append(ssb)
+            if g + 1 < NG:
                 codes = codes_next
 
-        add_partitions(NB - 1, ssb_prev)
+        add_partitions(NG - 1, ssbs[NG - 1])
         a_sb = const.tile([P, 512], F32)
         nc.vector.scalar_tensor_tensor(out=a_sb[:], in0=bsum[:], scalar=512.0, in1=pa[:], op0=MULT, op1=ADD)
         nc.sync.dma_start(out=out_3, in_=a_sb[0:8, :])

@@ -21,6 +21,7 @@ QM, QP, PM, PP = 16, 20, 24, 28
 
 ROFPOS = [0, 6, 4, 2, 1, 7, 5, 3, 8, 10, 9, 11]
 WM, HM, WP, HP, ZZ = 0, 256, 512, 768, 1024
+SLOTS = [1, 2, 0, 3]
 
 
 def tile_modelnew_pa_t_kernel(tc, x, w1, b1, out_0, out_1, out_2, out_3):
@@ -34,21 +35,25 @@ def tile_modelnew_pa_t_kernel(tc, x, w1, b1, out_0, out_1, out_2, out_3):
         name="pap", bufs=1
     ) as pap, tc.psum_pool(name="mm", bufs=5) as mmp:
         brow = const.tile([P, 1536], BF16)
-        nc.gpsimd.memset(brow[:], 0.0)
-        nc.sync.dma_start(out=brow[0:1, :], in_=b1.unsqueeze(0))
+        nc.vector.memset(brow[:], 0.0)
         raw = xpool.tile([P, NB, 2048], BF16)
         w_sb = wpool.tile([P, 12 * 512], BF16)
 
         def load_x(b):
             nc.sync.dma_start(out=raw[:, b, :], in_=x[b].rearrange("(p j) w h -> p (j w h)", j=4))
 
-        for b in range(4):
-            load_x(b)
-        for i in range(3):
+        def load_w(i):
             nc.sync.dma_start(
                 out=w_sb[:, i * 2048 : (i + 1) * 2048].rearrange("p (r k) -> p r k", k=512),
                 in_=w1[i * 512 : (i + 1) * 512, :].rearrange("(r p) k -> p r k", p=P),
             )
+
+        load_w(2)
+        for b in range(4):
+            load_x(b)
+        nc.sync.dma_start(out=brow[0:1, :], in_=b1.unsqueeze(0))
+        load_w(0)
+        load_w(1)
         for b in range(4, NB):
             load_x(b)
 
@@ -62,16 +67,31 @@ def tile_modelnew_pa_t_kernel(tc, x, w1, b1, out_0, out_1, out_2, out_3):
             for b4 in range(4):
                 nc.gpsimd.memset(pick[32 * b4 : 32 * b4 + 32, g, 4 * g + b4 : 4 * g + b4 + 1], 1.0)
 
+        w32 = w_sb[:].bitcast(F32).rearrange("p (r q u) -> p r u q", r=12, u=2)
+        gw = wpool.tile([P, 6144], BF16, align_bytes=64)
+        gw32 = gw[:].bitcast(F32).rearrange("p (i r o u) -> p i r o u", i=6, r=2, u=2)
+        wcodes = wpool.tile([P, 1536], U32, align_bytes=64)
+        wscales = wpool.tile([P, 1536], U8, align_bytes=64)
+
+        def wprep(h):
+            for i in (2 * h, 2 * h + 1):
+                pt = mmp.tile([P, 2, 2, P], F32, tag="mm")
+                for rr in range(2):
+                    for u in range(2):
+                        nc.tensor.transpose(pt[:, rr, u, :], w32[:, ROFPOS[2 * i + rr], u, :], ident[:])
+                nc.scalar.copy(out=gw32[:, i], in_=pt[:].rearrange("p r u o -> p r o u"))
+            nc.vector.quantize_mx(
+                out=wcodes[:, h * 512 : (h + 1) * 512].bitcast(FP8X4),
+                scales=wscales[:, h * 512 : (h + 1) * 512],
+                in_=gw[:, h * 2048 : (h + 1) * 2048],
+            )
+
         def regroup(gt, b, copy):
             b4 = b % 4
             copy(
                 out=gt[:, :, :, 32 * b4 : 32 * b4 + 32, :].rearrange("p v r (q i) j -> p r q v i j", q=4),
                 in_=raw[:, b, :].rearrange("p (j q v i r) -> p r q v i j", j=4, q=4, v=4, i=8),
             )
-
-        def new_group():
-            gt = gpool.tile([P, 4, 4, P, 4], BF16, align_bytes=64, tag="g")
-            return gt
 
         def quantise(gt):
             xc = cpool.tile([P, 32 * P], U32, align_bytes=64, tag="xc")
@@ -84,7 +104,7 @@ def tile_modelnew_pa_t_kernel(tc, x, w1, b1, out_0, out_1, out_2, out_3):
                 )
             return xc, xs
 
-        def move(flat, i):
+        def move_w(flat, i):
             mv = nc.vector.tensor_copy
             n = 16 * i
             bq = flat[:, 0 : 16 * n].rearrange("p (v r b q i) -> p v r b q i", v=4, r=4, b=4, q=4)
@@ -109,44 +129,10 @@ def tile_modelnew_pa_t_kernel(tc, x, w1, b1, out_0, out_1, out_2, out_3):
             xc, xs = xcs
             move_h(xc[:].bitcast(I32))
             move_h(xs[:])
-            move(xc[:].bitcast(I32), 8)
-            move(xs[:].bitcast(I32), 2)
-
-        gt0 = new_group()
-        regroup(gt0, 0, nc.scalar.copy)
-        regroup(gt0, 1, nc.vector.tensor_copy)
-        regroup(gt0, 2, nc.scalar.copy)
-        regroup(gt0, 3, nc.vector.tensor_copy)
-        codes = quantise(gt0)
-        moves(codes)
+            move_w(xc[:].bitcast(I32), 8)
+            move_w(xs[:].bitcast(I32), 2)
 
         bias = const.tile([P, 1536], F32)
-        for i in range(3):
-            pb = mmp.tile([P, 512], F32, tag="mm")
-            nc.tensor.matmul(pb[:], lhsT=ones_bf[:], rhs=brow[:, i * 512 : (i + 1) * 512], start=True, stop=True)
-            nc.scalar.copy(out=bias[:, i * 512 : (i + 1) * 512], in_=pb[:])
-        bsum = const.tile([P, 512], F32)
-        nc.gpsimd.tensor_tensor(out=bsum[:], in0=bias[:, 0:512], in1=bias[:, 512:1024], op=ADD)
-        nc.gpsimd.tensor_tensor(out=bsum[:], in0=bsum[:], in1=bias[:, 1024:1536], op=ADD)
-
-        w32 = w_sb[:].bitcast(F32).rearrange("p (r q u) -> p r u q", r=12, u=2)
-        gw = wpool.tile([P, 6144], BF16, align_bytes=64)
-        gw32 = gw[:].bitcast(F32).rearrange("p (i r o u) -> p i r o u", i=6, r=2, u=2)
-        wcodes = wpool.tile([P, 1536], U32, align_bytes=64)
-        wscales = wpool.tile([P, 1536], U8, align_bytes=64)
-        for i in range(6):
-            pt = mmp.tile([P, 2, 2, P], F32, tag="mm")
-            for rr in range(2):
-                for u in range(2):
-                    nc.tensor.transpose(pt[:, rr, u, :], w32[:, ROFPOS[2 * i + rr], u, :], ident[:])
-            nc.scalar.copy(out=gw32[:, i], in_=pt[:].rearrange("p r u o -> p r o u"))
-            if i % 2 == 1:
-                h = i // 2
-                nc.vector.quantize_mx(
-                    out=wcodes[:, h * 512 : (h + 1) * 512].bitcast(FP8X4),
-                    scales=wscales[:, h * 512 : (h + 1) * 512],
-                    in_=gw[:, h * 2048 : (h + 1) * 2048],
-                )
 
         def mx(out, xcs, t, col, n, start, stop):
             nc.tensor.matmul_mx(
@@ -160,100 +146,133 @@ def tile_modelnew_pa_t_kernel(tc, x, w1, b1, out_0, out_1, out_2, out_3):
             )
 
         def store(k, g, v, st):
-            if k == 1:
-                dst = outs[k][4 * g : 4 * g + 4].rearrange("b (q v) h c -> v (b q) (h c)", v=4)[v]
-            else:
-                dst = outs[k][4 * g : 4 * g + 4].rearrange("b (q v) (i o) c -> v (b q) i (o c)", v=4, o=4)[v]
+            dst = outs[k][4 * g : 4 * g + 4].rearrange("b (q v) (i o) c -> v (b q) i (o c)", v=4, o=4)[v]
             nc.sync.dma_start(out=dst, in_=st[:].rearrange("p o c -> p (o c)"))
+
+        def shifted(v, r):
+            wm = (v - 1) * 4 + r if v > 0 else QM + r
+            wp = (v + 1) * 4 + r if v < 3 else QP + r
+            hm = v * 4 + r - 1 if r > 0 else PM + v
+            hp = v * 4 + r + 1 if r < 3 else PP + v
+            return wm, wp, hm, hp
+
+        def bank1(codes, ssum, st, v, r):
+            wm, wp, hm, hp = shifted(v, r)
+            pm = mmp.tile([P, 512], F32, tag="mm")
+            mx(pm[:, 0:128], codes, wm, WM, 128, True, True)
+            mx(ssum[:, 0:256], codes, wm, WM, 256, False, False)
+            mx(pm[:, 128:256], codes, wp, WP, 128, True, True)
+            mx(ssum[:, 256:512], codes, wp, WP, 256, False, False)
+            mx(pm[:, 256:384], codes, hm, HM + 128, 128, True, True)
+            mx(pm[:, 384:512], codes, hp, HP + 128, 128, True, True)
+            nc.vector.tensor_tensor(out=st[:, r, :], in0=pm[:], in1=bias[:, 0:512], op=ADD)
+
+        def bank2(codes, ssum, st, v, r):
+            wm, wp, hm, hp = shifted(v, r)
+            pm = mmp.tile([P, 512], F32, tag="mm")
+            mx(pm[:, 0:128], codes, hm, HM, 128, True, True)
+            mx(ssum[:, 0:256], codes, hm, HM, 256, False, False)
+            mx(pm[:, 128:256], codes, hp, HP, 128, True, True)
+            mx(ssum[:, 256:512], codes, hp, HP, 256, False, False)
+            mx(pm[:, 256:384], codes, wm, WM + 128, 128, True, True)
+            mx(pm[:, 384:512], codes, wp, WP + 128, 128, True, True)
+            nc.vector.tensor_tensor(out=st[:, r, :], in0=pm[:], in1=bias[:, 512:1024], op=ADD)
+
+        def bank3(codes, ssum, st, v, r, flags, on_vector):
+            pm = mmp.tile([P, 512], F32, tag="mm")
+            mx(pm[:], codes, v * 4 + r, ZZ, 512, True, True)
+            if flags is not None:
+                mx(ssum[:], codes, v * 4 + r, ZZ, 512, flags[0], flags[1])
+            natural = st[:, r, :].rearrange("p (a b c) -> p a b c", a=2, b=2)
+            swapped = pm[:].rearrange("p (a b c) -> p b a c", a=2, b=2)
+            if on_vector:
+                nc.vector.tensor_tensor(
+                    out=natural,
+                    in0=swapped,
+                    in1=bias[:, 1024:1536].rearrange("p (a b c) -> p a b c", a=2, b=2),
+                    op=ADD,
+                )
+            else:
+                nc.scalar.copy(out=natural, in_=swapped)
+                nc.gpsimd.tensor_tensor(out=st[:, r, :], in0=st[:, r, :], in1=bias[:, 1024:1536], op=ADD)
 
         pa = pap.tile([P, 512], F32)
 
-        def add_partitions(g, ssb):
-            nc.tensor.matmul(pa[:], lhsT=pick[:, g, :], rhs=ssb[:], start=(g == 0), stop=(g == NG - 1))
-
-        SLOTS = [1, 2, 0, 3]
-        ssbs = []
-        for g in range(NG):
-            ssum = accp.tile([P, 512], F32, tag="ss")
-            mx(ssum[:], codes, SLOTS[0] * 4, ZZ, 512, True, False)
-
-            def bank1(st, v, r):
-                wm = (v - 1) * 4 + r if v > 0 else QM + r
-                wp = (v + 1) * 4 + r if v < 3 else QP + r
-                hm = v * 4 + r - 1 if r > 0 else PM + v
-                hp = v * 4 + r + 1 if r < 3 else PP + v
-                pm = mmp.tile([P, 512], F32, tag="mm")
-                mx(pm[:, 0:128], codes, wm, WM, 128, True, True)
-                mx(ssum[:, 0:256], codes, wm, WM, 256, False, False)
-                mx(pm[:, 128:256], codes, wp, WP, 128, True, True)
-                mx(ssum[:, 256:512], codes, wp, WP, 256, False, False)
-                mx(pm[:, 256:384], codes, hm, HM + 128, 128, True, True)
-                mx(pm[:, 384:512], codes, hp, HP + 128, 128, True, True)
-                nc.vector.tensor_tensor(out=st[:, r, :], in0=pm[:], in1=bias[:, 0:512], op=ADD)
-
-            def bank2(st, v, r):
-                wm = (v - 1) * 4 + r if v > 0 else QM + r
-                wp = (v + 1) * 4 + r if v < 3 else QP + r
-                hm = v * 4 + r - 1 if r > 0 else PM + v
-                hp = v * 4 + r + 1 if r < 3 else PP + v
-                pm = mmp.tile([P, 512], F32, tag="mm")
-                mx(pm[:, 0:128], codes, hm, HM, 128, True, True)
-                mx(ssum[:, 0:256], codes, hm, HM, 256, False, False)
-                mx(pm[:, 128:256], codes, hp, HP, 128, True, True)
-                mx(ssum[:, 256:512], codes, hp, HP, 256, False, False)
-                mx(pm[:, 256:384], codes, wm, WM + 128, 128, True, True)
-                mx(pm[:, 384:512], codes, wp, WP + 128, 128, True, True)
-                nc.vector.tensor_tensor(out=st[:, r, :], in0=pm[:], in1=bias[:, 512:1024], op=ADD)
-
-            def bank3(st, v, r, first, last):
-                pm = mmp.tile([P, 512], F32, tag="mm")
-                mx(pm[:], codes, v * 4 + r, ZZ, 512, True, True)
-                if not first:
-                    mx(ssum[:], codes, v * 4 + r, ZZ, 512, False, last)
-                nc.scalar.copy(
-                    out=st[:, r, :].rearrange("p (a b c) -> p a b c", a=2, b=2),
-                    in_=pm[:].rearrange("p (a b c) -> p b a c", a=2, b=2),
-                )
-                nc.gpsimd.tensor_tensor(out=st[:, r, :], in0=st[:, r, :], in1=bias[:, 1024:1536], op=ADD)
-
-            for n, v in enumerate(SLOTS):
-                st1 = stage.tile([P, 4, 512], F32, tag="st")
-                st3 = stage.tile([P, 4, 512], F32, tag="st")
-                bank1(st1, v, 0)
-                bank3(st3, v, 0, n == 0, False)
-                bank1(st1, v, 1)
-                bank1(st1, v, 2)
-                bank3(st3, v, 1, False, False)
-                bank1(st1, v, 3)
-                store(0, g, v, st1)
-                st2 = stage.tile([P, 4, 512], F32, tag="st")
-                bank2(st2, v, 0)
-                bank3(st3, v, 2, False, False)
-                bank2(st2, v, 1)
-                bank2(st2, v, 2)
-                bank2(st2, v, 3)
-                store(1, g, v, st2)
-                bank3(st3, v, 3, False, n == 3)
-                store(2, g, v, st3)
-                if g + 1 < NG and n == 0:
-                    gt1 = new_group()
-                    for b in range(4, NB):
-                        regroup(gt1, b, nc.scalar.copy)
-                if g + 1 < NG and n == 2:
-                    codes_next = quantise(gt1)
-                    moves(codes_next)
-                if g > 0 and n == 0:
-                    add_partitions(g - 1, ssbs[g - 1])
+        def add_partitions(g, ssum):
             ssb = sums.tile([P, 512], F32, tag="ssb")
             nc.scalar.copy(
                 out=ssb[:].rearrange("p (a b c) -> p a b c", a=2, b=2),
                 in_=ssum[:].rearrange("p (a b c) -> p b a c", a=2, b=2),
             )
-            ssbs.append(ssb)
-            if g + 1 < NG:
-                codes = codes_next
+            nc.tensor.matmul(pa[:], lhsT=pick[:, g, :], rhs=ssb[:], start=(g == 0), stop=(g == NG - 1))
 
-        add_partitions(NG - 1, ssbs[NG - 1])
+        wprep(2)
+        gt0 = gpool.tile([P, 4, 4, P, 4], BF16, align_bytes=64, tag="g")
+        regroup(gt0, 0, nc.scalar.copy)
+        regroup(gt0, 1, nc.vector.tensor_copy)
+        regroup(gt0, 2, nc.vector.tensor_copy)
+        regroup(gt0, 3, nc.vector.tensor_copy)
+        for i in (2, 0, 1):
+            pb = mmp.tile([P, 512], F32, tag="mm")
+            nc.tensor.matmul(pb[:], lhsT=ones_bf[:], rhs=brow[:, i * 512 : (i + 1) * 512], start=True, stop=True)
+            nc.scalar.copy(out=bias[:, i * 512 : (i + 1) * 512], in_=pb[:])
+        codes0 = quantise(gt0)
+        ssum0 = accp.tile([P, 512], F32, tag="ss")
+        for v in range(4):
+            st3 = stage.tile([P, 4, 512], F32, tag="st")
+            for r in range(4):
+                flags = None if (v, r) == (3, 3) else ((v, r) == (0, 0), False)
+                bank3(codes0, ssum0, st3, v, r, flags, r % 2 == 0)
+            store(2, 0, v, st3)
+            if v == 0:
+                wprep(0)
+            if v == 1:
+                wprep(1)
+                moves(codes0)
+        bsum = const.tile([P, 512], F32)
+        nc.gpsimd.tensor_tensor(out=bsum[:], in0=bias[:, 0:512], in1=bias[:, 512:1024], op=ADD)
+        nc.gpsimd.tensor_tensor(out=bsum[:], in0=bsum[:], in1=bias[:, 1024:1536], op=ADD)
+        gt1 = gpool.tile([P, 4, 4, P, 4], BF16, align_bytes=64, tag="g")
+        for b in range(4, NB):
+            regroup(gt1, b, nc.scalar.copy)
+        for n, v in enumerate(SLOTS):
+            st1 = stage.tile([P, 4, 512], F32, tag="st")
+            for r in range(4):
+                bank1(codes0, ssum0, st1, v, r)
+            store(0, 0, v, st1)
+            st2 = stage.tile([P, 4, 512], F32, tag="st")
+            for r in range(4):
+                bank2(codes0, ssum0, st2, v, r)
+            store(1, 0, v, st2)
+            if n == 1:
+                codes1 = quantise(gt1)
+                moves(codes1)
+        mx(ssum0[:], codes0, 15, ZZ, 512, False, True)
+
+        ssum1 = accp.tile([P, 512], F32, tag="ss")
+        for n, v in enumerate(SLOTS):
+            st1 = stage.tile([P, 4, 512], F32, tag="st")
+            st3 = stage.tile([P, 4, 512], F32, tag="st")
+            bank3(codes1, ssum1, st3, v, 0, (n == 0, False), False)
+            bank1(codes1, ssum1, st1, v, 0)
+            bank1(codes1, ssum1, st1, v, 1)
+            bank3(codes1, ssum1, st3, v, 1, (False, False), False)
+            bank1(codes1, ssum1, st1, v, 2)
+            bank1(codes1, ssum1, st1, v, 3)
+            store(0, 1, v, st1)
+            st2 = stage.tile([P, 4, 512], F32, tag="st")
+            bank2(codes1, ssum1, st2, v, 0)
+            bank3(codes1, ssum1, st3, v, 2, (False, False), False)
+            bank2(codes1, ssum1, st2, v, 1)
+            bank2(codes1, ssum1, st2, v, 2)
+            bank2(codes1, ssum1, st2, v, 3)
+            store(1, 1, v, st2)
+            bank3(codes1, ssum1, st3, v, 3, (False, n == 3), False)
+            store(2, 1, v, st3)
+            if n == 0:
+                add_partitions(0, ssum0)
+
+        add_partitions(1, ssum1)
         a_sb = const.tile([P, 512], F32)
         nc.vector.scalar_tensor_tensor(out=a_sb[:], in0=bsum[:], scalar=512.0, in1=pa[:], op0=MULT, op1=ADD)
         nc.sync.dma_start(out=out_3, in_=a_sb[0:8, :])

import concourse.mybir as mybir
from concourse.masks import make_identity

FP8X4 = mybir.dt.float8_e4m3fn_x4
BF16 = mybir.dt.bfloat16
F32 = mybir.dt.float32
U32 = mybir.dt.uint32
U8 = mybir.dt.uint8
I32 = mybir.dt.int32
ADD = mybir.AluOpType.add
MULT = mybir.AluOpType.mult

P = 128
FLOPS = 2 * 4096 * 512 * 1536

NB = 8
NG = 2
NSTAGE = 10

QM, QP, PM, PP = 16, 20, 24, 28

ROFPOS = [0, 6, 4, 2, 1, 7, 5, 3, 8, 10, 9, 11]
WM, HM, WP, HP, ZZ = 0, 256, 512, 768, 1024
SLOTS = [1, 2, 0, 3]


def tile_modelnew_pa_t_kernel(tc, x, w1, b1, out_0, out_1, out_2, out_3):
    nc = tc.nc
    outs = [out_0, out_1, out_2]
    with tc.tile_pool(name="const", bufs=1) as const, tc.tile_pool(name="wpool", bufs=1) as wpool, tc.tile_pool(
        name="xpool", bufs=1
    ) as xpool, tc.tile_pool(name="gpool", bufs=1) as gpool, tc.tile_pool(name="cpool", bufs=2) as cpool, tc.tile_pool(
        name="sums", bufs=2
    ) as sums, tc.tile_pool(name="stage", bufs=NSTAGE) as stage, tc.psum_pool(name="acc", bufs=2) as accp, tc.psum_pool(
        name="pap", bufs=1
    ) as pap, tc.psum_pool(name="mm", bufs=5) as mmp:
        brow = const.tile([P, 1536], BF16)
        nc.vector.memset(brow[:], 0.0)
        raw = xpool.tile([P, NB, 2048], BF16)
        w_sb = wpool.tile([P, 12 * 512], BF16)

        def load_x(b):
            nc.sync.dma_start(out=raw[:, b, :], in_=x[b].rearrange("(p j) w h -> p (j w h)", j=4))

        def load_w(i):
            nc.sync.dma_start(
                out=w_sb[:, i * 2048 : (i + 1) * 2048].rearrange("p (r k) -> p r k", k=512),
                in_=w1[i * 512 : (i + 1) * 512, :].rearrange("(r p) k -> p r k", p=P),
            )

        load_w(2)
        for b in range(4):
            load_x(b)
        nc.sync.dma_start(out=brow[0:1, :], in_=b1.unsqueeze(0))
        load_w(0)
        load_w(1)
        for b in range(4, NB):
            load_x(b)

        ident = const.tile([P, P], F32)
        make_identity(nc, ident[:])
        ones_bf = const.tile([P, P], BF16)
        nc.vector.memset(ones_bf[:], 1.0)
        pick = const.tile([P, NG, P], F32)
        nc.gpsimd.memset(pick[:], 0.0)
        for g in range(NG):
            for b4 in range(4):
                nc.gpsimd.memset(pick[32 * b4 : 32 * b4 + 32, g, 4 * g + b4 : 4 * g + b4 + 1], 1.0)

        w32 = w_sb[:].bitcast(F32).rearrange("p (r q u) -> p r u q", r=12, u=2)
        gw = wpool.tile([P, 6144], BF16, align_bytes=64)
        gw32 = gw[:].bitcast(F32).rearrange("p (i r o u) -> p i r o u", i=6, r=2, u=2)
        wcodes = wpool.tile([P, 1536], U32, align_bytes=64)
        wscales = wpool.tile([P, 1536], U8, align_bytes=64)

        def wprep(h):
            for i in (2 * h, 2 * h + 1):
                pt = mmp.tile([P, 2, 2, P], F32, tag="mm")
                for rr in range(2):
                    for u in range(2):
                        nc.tensor.transpose(pt[:, rr, u, :], w32[:, ROFPOS[2 * i + rr], u, :], ident[:])
                nc.scalar.copy(out=gw32[:, i], in_=pt[:].rearrange("p r u o -> p r o u"))
            nc.vector.quantize_mx(
                out=wcodes[:, h * 512 : (h + 1) * 512].bitcast(FP8X4),
                scales=wscales[:, h * 512 : (h + 1) * 512],
                in_=gw[:, h * 2048 : (h + 1) * 2048],
            )

        def regroup(gt, b, copy):
            b4 = b % 4
            copy(
                out=gt[:, :, :, 32 * b4 : 32 * b4 + 32, :].rearrange("p v r (q i) j -> p r q v i j", q=4),
                in_=raw[:, b, :].rearrange("p (j q v i r) -> p r q v i j", j=4, q=4, v=4, i=8),
            )

        def quantise(gt):
            xc = cpool.tile([P, 32 * P], U32, align_bytes=64, tag="xc")
            xs = cpool.tile([P, 32 * P], U8, align_bytes=64, tag="xs")
            for v in range(4):
                nc.vector.quantize_mx(
                    out=xc[:, v * 512 : (v + 1) * 512].bitcast(FP8X4),
                    scales=xs[:, v * 512 : (v + 1) * 512],
                    in_=gt[:, v].rearrange("p r m j -> p (r m j)"),
                )
            return xc, xs

        def move_w(flat, i):
            mv = nc.vector.tensor_copy
            n = 16 * i
            bq = flat[:, 0 : 16 * n].rearrange("p (v r b q i) -> p v r b q i", v=4, r=4, b=4, q=4)
            qm = flat[:, QM * n : (QM + 4) * n].rearrange("p (r b q i) -> p r b q i", r=4, b=4, q=4)
            qp = flat[:, QP * n : (QP + 4) * n].rearrange("p (r b q i) -> p r b q i", r=4, b=4, q=4)
            mv(out=qm[:, :, :, 1:4, :], in_=bq[:, 3, :, :, 0:3, :])
            mv(out=qm[:, :, :, 0, :], in_=bq[:, 0, :, :, 0, :])
            mv(out=qp[:, :, :, 0:3, :], in_=bq[:, 0, :, :, 1:4, :])
            mv(out=qp[:, :, :, 3, :], in_=bq[:, 3, :, :, 3, :])

        def move_h(flat):
            mv = nc.vector.tensor_copy
            bi = flat[:, 0 : 16 * P].rearrange("p (v r m i) -> p v r m i", v=4, r=4, i=8)
            pm = flat[:, PM * P : (PM + 4) * P].rearrange("p (v m i) -> p v m i", v=4, i=8)
            pp = flat[:, PP * P : (PP + 4) * P].rearrange("p (v m i) -> p v m i", v=4, i=8)
            mv(out=pm[:, :, :, 1:8], in_=bi[:, :, 3, :, 0:7])
            mv(out=pm[:, :, :, 0], in_=bi[:, :, 0, :, 0])
            mv(out=pp[:, :, :, 0:7], in_=bi[:, :, 0, :, 1:8])
            mv(out=pp[:, :, :, 7], in_=bi[:, :, 3, :, 7])

        def moves(xcs):
            xc, xs = xcs
            move_h(xc[:].bitcast(I32))
            move_h(xs[:])
            move_w(xc[:].bitcast(I32), 8)
            move_w(xs[:].bitcast(I32), 2)

        bias = const.tile([P, 1536], F32)

        def mx(out, xcs, t, col, n, start, stop):
            nc.tensor.matmul_mx(
                out=out,
                lhsT=xcs[0][:, t * P : (t + 1) * P].bitcast(FP8X4),
                lhsT_scale=xcs[1][:, t * P : (t + 1) * P],
                rhs=wcodes[:, col : col + n].bitcast(FP8X4),
                rhs_scale=wscales[:, col : col + n],
                start=start,
                stop=stop,
            )

        def store(k, g, v, st):
            dst = outs[k][4 * g : 4 * g + 4].rearrange("b (q v) (i o) c -> v (b q) i (o c)", v=4, o=4)[v]
            nc.sync.dma_start(out=dst, in_=st[:].rearrange("p o c -> p (o c)"))

        def shifted(v, r):
            wm = (v - 1) * 4 + r if v > 0 else QM + r
            wp = (v + 1) * 4 + r if v < 3 else QP + r
            hm = v * 4 + r - 1 if r > 0 else PM + v
            hp = v * 4 + r + 1 if r < 3 else PP + v
            return wm, wp, hm, hp

        def bank1(codes, ssum, st, v, r):
            wm, wp, hm, hp = shifted(v, r)
            pm = mmp.tile([P, 512], F32, tag="mm")
            mx(pm[:, 0:128], codes, wm, WM, 128, True, True)
            mx(ssum[:, 0:256], codes, wm, WM, 256, False, False)
            mx(pm[:, 128:256], codes, wp, WP, 128, True, True)
            mx(ssum[:, 256:512], codes, wp, WP, 256, False, False)
            mx(pm[:, 256:384], codes, hm, HM + 128, 128, True, True)
            mx(pm[:, 384:512], codes, hp, HP + 128, 128, True, True)
            nc.vector.tensor_tensor(out=st[:, r, :], in0=pm[:], in1=bias[:, 0:512], op=ADD)

        def bank2(codes, ssum, st, v, r):
            wm, wp, hm, hp = shifted(v, r)
            pm = mmp.tile([P, 512], F32, tag="mm")
            mx(pm[:, 0:128], codes, hm, HM, 128, True, True)
            mx(ssum[:, 0:256], codes, hm, HM, 256, False, False)
            mx(pm[:, 128:256], codes, hp, HP, 128, True, True)
            mx(ssum[:, 256:512], codes, hp, HP, 256, False, False)
            mx(pm[:, 256:384], codes, wm, WM + 128, 128, True, True)
            mx(pm[:, 384:512], codes, wp, WP + 128, 128, True, True)
            nc.vector.tensor_tensor(out=st[:, r, :], in0=pm[:], in1=bias[:, 512:1024], op=ADD)

        def bank3(codes, ssum, st, v, r, flags, on_vector):
            pm = mmp.tile([P, 512], F32, tag="mm")
            mx(pm[:], codes, v * 4 + r, ZZ, 512, True, True)
            if flags is not None:
                mx(ssum[:], codes, v * 4 + r, ZZ, 512, flags[0], flags[1])
            natural = st[:, r, :].rearrange("p (a b c) -> p a b c", a=2, b=2)
            swapped = pm[:].rearrange("p (a b c) -> p b a c", a=2, b=2)
            if on_vector:
                nc.vector.tensor_tensor(
                    out=natural,
                    in0=swapped,
                    in1=bias[:, 1024:1536].rearrange("p (a b c) -> p a b c", a=2, b=2),
                    op=ADD,
                )
            else:
                nc.scalar.copy(out=natural, in_=swapped)
                nc.gpsimd.tensor_tensor(out=st[:, r, :], in0=st[:, r, :], in1=bias[:, 1024:1536], op=ADD)

        pa = pap.tile([P, 512], F32)

        def add_partitions(g, ssum):
            ssb = sums.tile([P, 512], F32, tag="ssb")
            nc.scalar.copy(
                out=ssb[:].rearrange("p (a b c) -> p a b c", a=2, b=2),
                in_=ssum[:].rearrange("p (a b c) -> p b a c", a=2, b=2),
            )
            nc.tensor.matmul(pa[:], lhsT=pick[:, g, :], rhs=ssb[:], start=(g == 0), stop=(g == NG - 1))

        wprep(2)
        gt0 = gpool.tile([P, 4, 4, P, 4], BF16, align_bytes=64, tag="g")
        regroup(gt0, 0, nc.scalar.copy)
        regroup(gt0, 1, nc.vector.tensor_copy)
        regroup(gt0, 2, nc.vector.tensor_copy)
        regroup(gt0, 3, nc.vector.tensor_copy)
        for i in (2, 0, 1):
            pb = mmp.tile([P, 512], F32, tag="mm")
            nc.tensor.matmul(pb[:], lhsT=ones_bf[:], rhs=brow[:, i * 512 : (i + 1) * 512], start=True, stop=True)
            nc.scalar.copy(out=bias[:, i * 512 : (i + 1) * 512], in_=pb[:])
        codes0 = quantise(gt0)
        ssum0 = accp.tile([P, 512], F32, tag="ss")
        for v in range(4):
            st3 = stage.tile([P, 4, 512], F32, tag="st")
            for r in range(4):
                flags = None if (v, r) == (3, 3) else ((v, r) == (0, 0), False)
                bank3(codes0, ssum0, st3, v, r, flags, r % 2 == 0)
            store(2, 0, v, st3)
            if v == 0:
                wprep(0)
            if v == 1:
                wprep(1)
                moves(codes0)
        bsum = const.tile([P, 512], F32)
        nc.gpsimd.tensor_tensor(out=bsum[:], in0=bias[:, 0:512], in1=bias[:, 512:1024], op=ADD)
        nc.gpsimd.tensor_tensor(out=bsum[:], in0=bsum[:], in1=bias[:, 1024:1536], op=ADD)
        gt1 = gpool.tile([P, 4, 4, P, 4], BF16, align_bytes=64, tag="g")
        for b in range(4, NB):
            regroup(gt1, b, nc.scalar.copy)
        for n, v in enumerate(SLOTS):
            st1 = stage.tile([P, 4, 512], F32, tag="st")
            for r in range(4):
                bank1(codes0, ssum0, st1, v, r)
            store(0, 0, v, st1)
            st2 = stage.tile([P, 4, 512], F32, tag="st")
            for r in range(4):
                bank2(codes0, ssum0, st2, v, r)
            store(1, 0, v, st2)
            if n == 1:
                codes1 = quantise(gt1)
                moves(codes1)
        mx(ssum0[:], codes0, 15, ZZ, 512, False, True)

        ssum1 = accp.tile([P, 512], F32, tag="ss")
        for n, v in enumerate(SLOTS):
            st1 = stage.tile([P, 4, 512], F32, tag="st")
            st3 = stage.tile([P, 4, 512], F32, tag="st")
            bank3(codes1, ssum1, st3, v, 0, (n == 0, False), False)
            bank1(codes1, ssum1, st1, v, 0)
            bank1(codes1, ssum1, st1, v, 1)
            bank3(codes1, ssum1, st3, v, 1, (False, False), False)
            bank1(codes1, ssum1, st1, v, 2)
            bank1(codes1, ssum1, st1, v, 3)
            store(0, 1, v, st1)
            st2 = stage.tile([P, 4, 512], F32, tag="st")
            bank2(codes1, ssum1, st2, v, 0)
            bank3(codes1, ssum1, st3, v, 2, (False, False), False)
            bank2(codes1, ssum1, st2, v, 1)
            bank2(codes1, ssum1, st2, v, 2)
            bank2(codes1, ssum1, st2, v, 3)
            store(1, 1, v, st2)
            bank3(codes1, ssum1, st3, v, 3, (False, n == 3), False)
            store(2, 1, v, st3)
            if n == 0:
                add_partitions(0, ssum0)

        add_partitions(1, ssum1)
        a_sb = const.tile([P, 512], F32)
        nc.vector.scalar_tensor_tensor(out=a_sb[:], in0=bsum[:], scalar=512.0, in1=pa[:], op0=MULT, op1=ADD)
        nc.sync.dma_start(out=out_3, in_=a_sb[0:8, :])
